import numpy as np
import ml_dtypes


def mxq(x, axis, fmt="e4m3"):
    dtype, down = {"e4m3": (ml_dtypes.float8_e4m3fn, 7), "e5m2": (ml_dtypes.float8_e5m2, 14)}[fmt]
    v = np.moveaxis(np.asarray(x, np.float32).astype(ml_dtypes.bfloat16).astype(np.float64), axis, -1)
    blocks = v.reshape(v.shape[:-1] + (-1, 32))
    amax = np.abs(blocks).max(-1, keepdims=True)
    byte = np.maximum(np.where(amax > 0, np.frexp(amax)[1] - 1 + 127, 0) - down, 1)
    scale = np.exp2(byte - 127.0)
    codes = (blocks / scale).astype(np.float32).astype(dtype).astype(np.float64)
    return np.moveaxis((codes * scale).reshape(v.shape), -1, axis)


WIDE = False


def mx_kscale(k):
    if not WIDE:
        return np.ones(k)
    levels = np.array([10, -10, 5, -5, 0])
    a = np.random.permutation(np.resize(levels, k // 512 * 4)).reshape(k // 512, 4)
    idx = np.arange(k)
    return np.exp2(a[idx // 512, idx % 128 // 32])


BF16 = ml_dtypes.bfloat16


def bf(x):
    return np.asarray(x, np.float32).astype(BF16)


def f64(x):
    return np.asarray(x).astype(np.float64)


E2M1 = np.array([0.0, 0.5, 1.0, 1.5, 2.0, 3.0, 4.0, 6.0, -0.0, -0.5, -1.0, -1.5, -2.0, -3.0, -4.0, -6.0])


def pack_weight(w, fmt):
    k, n = w.shape
    w = f64(bf(w)).reshape(k // 32, 32, n)
    amax = np.abs(w).max(1)
    if fmt == "e4m3":
        byte = np.frexp(amax)[1] - 1 + 127 - 7
    else:
        mant, ex = np.frexp(amax / 6.0)
        byte = np.where(mant > 0.5, ex, ex - 1) + 127
    byte = np.clip(np.where(amax > 0, byte, 1), 1, 254)
    scaled = (w * np.exp2(127.0 - byte)[:, None, :]).reshape(k, n).astype(np.float32)
    by_word = np.ascontiguousarray(scaled.reshape(k // 512, 128, 4, n).transpose(0, 1, 3, 2))
    if fmt == "e4m3":
        words = by_word.astype(ml_dtypes.float8_e4m3fn).view(np.uint8)
    else:
        c = by_word.astype(ml_dtypes.float4_e2m1fn).view(np.uint8) & 0xF
        words = c[..., 0::2] | (c[..., 1::2] << 4)
    return np.ascontiguousarray(words), np.ascontiguousarray(byte.astype(np.uint8).reshape(k // 512, 16, n))


def unpack_weight(words, scales, fmt):
    g, p, n, _ = words.shape
    if fmt == "e4m3":
        vals = np.ascontiguousarray(words).view(ml_dtypes.float8_e4m3fn).astype(np.float64)
    else:
        nib = np.empty((g, p, n, 4), np.uint8)
        nib[..., 0::2] = words & 0xF
        nib[..., 1::2] = words >> 4
        vals = E2M1[nib]
    vals = vals * np.repeat(np.exp2(scales.astype(np.float64) - 127.0), 8, axis=1)[..., None]
    return vals.transpose(0, 1, 3, 2).reshape(g * 512, n)


B, C_IN, C_OUT, N, T, K = 2, 512, 128, 512, 12, 3
FMT = 'e4m3'


def cheb_laplacian(p):
    adj = 1.0 / (1.0 + np.exp(-p))
    adj = (adj + adj.T) * 0.5
    adj = adj * (1.0 - np.eye(N))
    deg = adj.sum(axis=1)
    dis = 1.0 / np.sqrt(deg)
    return -(dis[:, None] * adj * dis[None, :])


def setup_inputs():
    s = mx_kscale(C_IN)
    x = np.random.standard_normal((B, C_IN, 1, T)) + np.random.standard_normal((B, C_IN, N, T))
    adj_param = bf(4.0 * np.random.standard_normal((N, N)) - 10.0 + 10.0 * np.eye(N))
    w_cheb0_words, w_cheb0_scales = pack_weight(np.random.standard_normal((C_IN, C_OUT)) / np.sqrt(C_IN) / s[:, None], FMT)
    w_cheb1_words, w_cheb1_scales = pack_weight(np.random.standard_normal((C_IN, C_OUT)) / np.sqrt(C_IN) / s[:, None], FMT)
    return {'x': bf(x * s[None, :, None, None]),
            'adj_param': adj_param,
            'w_cheb0_words': w_cheb0_words,
            'w_cheb0_scales': w_cheb0_scales,
            'w_cheb1_words': w_cheb1_words,
            'w_cheb1_scales': w_cheb1_scales}


def reference(x, adj_param, w_cheb0_words, w_cheb0_scales, w_cheb1_words, w_cheb1_scales):
    s = cheb_laplacian(f64(adj_param))
    xt = f64(x).transpose(0, 3, 2, 1)
    h = mxq(xt, 3, 'e4m3') @ unpack_weight(w_cheb0_words, w_cheb0_scales, FMT)
    tx1 = mxq(s, 1, 'e4m3') @ mxq(xt, 2, 'e4m3')
    h = h + (mxq(tx1, 3, 'e4m3') @ unpack_weight(w_cheb1_words, w_cheb1_scales, FMT))
    return h

@@ -1,0 +1,258 @@
+from contextlib import ExitStack
+
+import concourse.mybir as mybir
+from concourse.masks import make_identity
+
+BF16 = mybir.dt.bfloat16
+F32 = mybir.dt.float32
+I32 = mybir.dt.int32
+U32 = mybir.dt.uint32
+U8 = mybir.dt.uint8
+FP8X4 = mybir.dt.float8_e4m3fn_x4
+ACT = mybir.ActivationFunctionType
+ALU = mybir.AluOpType
+
+P = 128
+PACK = 4
+B, C, N, T, O = 2, 512, 512, 12, 128
+QUARTERS = N // P
+T_RUN = 4
+RUNS = T // T_RUN
+
+FLOPS = 2 * B * T * (N * N * C + 2 * N * C * O)
+
+
+def tile_dynamicgraphspatialconv_pa_t_kernel(
+    tc, x, adj_param, w_cheb0_words, w_cheb0_scales, w_cheb1_words, w_cheb1_scales, out
+):
+    nc = tc.nc
+    with ExitStack() as ctx:
+        keep = ctx.enter_context(tc.tile_pool(name="keep", bufs=1))
+        graph = ctx.enter_context(tc.tile_pool(name="graph", bufs=1))
+        raw_pool = ctx.enter_context(tc.tile_pool(name="raw", bufs=2))
+        stage = ctx.enter_context(tc.tile_pool(name="stage", bufs=3))
+        chan_pool = ctx.enter_context(tc.tile_pool(name="chan", bufs=3))
+        tx_pool = ctx.enter_context(tc.tile_pool(name="tx", bufs=2))
+        res_pool = ctx.enter_context(tc.tile_pool(name="res", bufs=3))
+        psum_t = ctx.enter_context(tc.psum_pool(name="psum_t", bufs=2))
+        psum_tx = ctx.enter_context(tc.psum_pool(name="psum_tx", bufs=4))
+        psum_h = ctx.enter_context(tc.psum_pool(name="psum_h", bufs=2))
+
+        ident_bf16 = keep.tile([P, P], BF16)
+        make_identity(nc, ident_bf16[:])
+        ident_f32 = keep.tile([P, P], F32)
+        make_identity(nc, ident_f32[:])
+
+        w_codes = keep.tile([P, 2, PACK * O], U8, align_bytes=64)
+        w_scales = keep.tile([P, 2, O], U8, align_bytes=64)
+        nc.vector.memset(w_scales[:].rearrange("p w o -> p (w o)").bitcast(I32), 0)
+        for w, (words, scales) in enumerate(
+            ((w_cheb0_words, w_cheb0_scales), (w_cheb1_words, w_cheb1_scales))
+        ):
+            nc.sync.dma_start(
+                out=w_codes[:, w, :].bitcast(I32),
+                in_=words[0].rearrange("p o j -> p (o j)").bitcast(I32),
+            )
+            for quadrant in range(4):
+                nc.sync.dma_start(
+                    out=w_scales[32 * quadrant : 32 * quadrant + 4, w, :].bitcast(I32),
+                    in_=scales[0, 4 * quadrant : 4 * quadrant + 4, :].bitcast(I32),
+                )
+
+        adj_sb = graph.tile([P, QUARTERS, N], BF16)
+        nc.sync.dma_start(out=adj_sb[:], in_=adj_param.rearrange("(k p) v -> p k v", p=P))
+        sig = graph.tile([P, QUARTERS, N], F32)
+        nc.scalar.activation(out=sig[:], in_=adj_sb[:], func=ACT.Sigmoid)
+        for k in range(QUARTERS):
+            diagonal_block = sig[:, k, k * P : (k + 1) * P]
+            nc.gpsimd.affine_select(
+                out=diagonal_block,
+                in_=diagonal_block,
+                compare_op=ALU.not_equal,
+                fill=0.0,
+                base=0,
+                pattern=[[-1, P]],
+                channel_multiplier=1,
+            )
+        sym = graph.tile([P, QUARTERS, N], F32)
+        row_sum = graph.tile([P, QUARTERS], F32)
+        for k in range(QUARTERS):
+            sig_t = psum_tx.tile([P, QUARTERS, P], F32, tag="bank")
+            for kv in range(QUARTERS):
+                nc.tensor.transpose(sig_t[:, kv, :], sig[:, kv, k * P : (k + 1) * P], ident_f32[:])
+            nc.vector.scalar_tensor_tensor(
+                out=sym[:, k, :],
+                in0=sig[:, k, :],
+                scalar=1.0,
+                in1=sig_t[:].rearrange("p k v -> p (k v)"),
+                op0=ALU.mult,
+                op1=ALU.add,
+                accum_out=row_sum[:, k : k + 1],
+            )
+        root = graph.tile([P, QUARTERS], F32)
+        nc.scalar.activation(out=root[:], in_=row_sum[:], func=ACT.Sqrt, scale=0.5)
+        dis = graph.tile([P, QUARTERS], F32)
+        nc.vector.reciprocal(out=dis[:], in_=root[:])
+        minus_half_dis = graph.tile([P, QUARTERS], F32)
+        nc.vector.tensor_scalar_mul(out=minus_half_dis[:], in0=dis[:], scalar1=-0.5)
+        dis_row = psum_h.tile([P, QUARTERS, P], F32, tag="acc")
+        for k in range(QUARTERS):
+            nc.tensor.matmul(
+                out=dis_row[:, k, :],
+                lhsT=dis[:, k : k + 1].to_broadcast([P, P]),
+                rhs=ident_f32[:],
+                start=True,
+                stop=True,
+            )
+        s_rows = graph.tile([P, QUARTERS, N], BF16)
+        for k in range(QUARTERS):
+            nc.vector.scalar_tensor_tensor(
+                out=s_rows[:, k, :],
+                in0=sym[:, k, :],
+                scalar=minus_half_dis[:, k : k + 1],
+                in1=dis_row[:].rearrange("p k v -> p (k v)"),
+                op0=ALU.mult,
+                op1=ALU.mult,
+            )
+        s_grouped = graph.tile([P, N, PACK], BF16, align_bytes=64)
+        nc.vector.tensor_copy(out=s_grouped[:], in_=s_rows[:].rearrange("p k v -> p v k"))
+        s_codes = keep.tile([P, N], U32, align_bytes=64)
+        s_scales = keep.tile([P, N], U8, align_bytes=64)
+        nc.vector.quantize_mx(
+            out=s_codes[:].bitcast(FP8X4),
+            scales=s_scales[:],
+            in_=s_grouped[:].rearrange("p v k -> p (v k)"),
+        )
+
+        node_codes = {}
+        node_scales = {}
+        for b in range(B):
+            for u in range(PACK):
+                node_codes[(b, u)] = keep.tile([P, T, P], U32, name="node_codes_%d_%d" % (b, u), align_bytes=64)
+                node_scales[(b, u)] = keep.tile([P, T, P], U8, name="node_scales_%d_%d" % (b, u), align_bytes=64)
+
+        def load_node_unit(b, u):
+            raw_n = raw_pool.tile([P, QUARTERS, P, T], BF16)
+            source = x[b].rearrange("(a ml u) (j n) t -> u a ml j (n t)", a=QUARTERS, u=PACK, j=QUARTERS)
+            for a in range(QUARTERS):
+                nc.sync.dma_start(out=raw_n[:, a, :, :].rearrange("p n t -> p (n t)"), in_=source[u, a])
+            return raw_n
+
+        def quantise_node_unit(raw_n, b, u, run):
+            grouped_n = stage.tile([P, T_RUN, PACK * P], BF16, align_bytes=64)
+            for half in range(2):
+                turned = psum_t.tile([P, 2, QUARTERS, P], BF16)
+                for i in range(2):
+                    t = T_RUN * run + 2 * half + i
+                    for a in range(QUARTERS):
+                        nc.tensor.transpose(turned[:, i, a, :], raw_n[:, a, :, t], ident_bf16[:])
+                nc.scalar.copy(
+                    out=grouped_n[:, 2 * half : 2 * half + 2, :],
+                    in_=turned[:].rearrange("p i a m -> p i (a m)"),
+                )
+            times = slice(T_RUN * run, T_RUN * (run + 1))
+            nc.vector.quantize_mx(
+                out=node_codes[(b, u)][:, times, :].rearrange("p t m -> p (t m)").bitcast(FP8X4),
+                scales=node_scales[(b, u)][:, times, :].rearrange("p t m -> p (t m)"),
+                in_=grouped_n[:].rearrange("p t m -> p (t m)"),
+            )
+
+        def load_channel_chunk(b, k):
+            raw_c = raw_pool.tile([P, PACK, P, T], BF16)
+            source = x[b].rearrange("(p j) (k n) t -> k p j (n t)", j=PACK, k=QUARTERS)
+            nc.sync.dma_start(out=raw_c[:].rearrange("p j n t -> p j (n t)"), in_=source[k])
+            chan_codes = chan_pool.tile([P, T, P], U32, align_bytes=64)
+            chan_scales = chan_pool.tile([P, T, P], U8, align_bytes=64)
+            return raw_c, chan_codes, chan_scales
+
+        def quantise_channel_chunk(chunk, run):
+            raw_c, chan_codes, chan_scales = chunk
+            times = slice(T_RUN * run, T_RUN * (run + 1))
+            grouped_c = stage.tile([P, T_RUN, P, PACK], BF16, align_bytes=64)
+            nc.vector.tensor_copy(
+                out=grouped_c[:].rearrange("p t n j -> p n j t"),
+                in_=raw_c[:, :, :, times].rearrange("p j n t -> p n j t"),
+            )
+            nc.vector.quantize_mx(
+                out=chan_codes[:, times, :].rearrange("p t n -> p (t n)").bitcast(FP8X4),
+                scales=chan_scales[:, times, :].rearrange("p t n -> p (t n)"),
+                in_=grouped_c[:].rearrange("p t n j -> p (t n j)"),
+            )
+
+        def convolve(b, k, run, chan_codes, chan_scales):
+            nodes = slice(k * P, (k + 1) * P)
+            grouped_x = stage.tile([P, T_RUN, P, PACK], BF16, align_bytes=64)
+            for i in range(T_RUN):
+                t = T_RUN * run + i
+                tx1_bank = psum_tx.tile([P, PACK, P], F32, tag="bank")
+                for u in range(PACK):
+                    nc.tensor.matmul_mx(
+                        out=tx1_bank[:, u, :],
+                        lhsT=node_codes[(b, u)][:, t, :].bitcast(FP8X4),
+                        lhsT_scale=node_scales[(b, u)][:, t, :],
+                        rhs=s_codes[:, nodes].bitcast(FP8X4),
+                        rhs_scale=s_scales[:, nodes],
+                        start=True,
+                        stop=True,
+                    )
+                nc.scalar.copy(out=grouped_x[:, i, :, :], in_=tx1_bank[:].rearrange("p u v -> p v u"))
+            tx1_codes = tx_pool.tile([P, T_RUN, P], U32, align_bytes=64)
+            tx1_scales = tx_pool.tile([P, T_RUN, P], U8, align_bytes=64)
+            nc.vector.quantize_mx(
+                out=tx1_codes[:].rearrange("p t v -> p (t v)").bitcast(FP8X4),
+                scales=tx1_scales[:].rearrange("p t v -> p (t v)"),
+                in_=grouped_x[:].rearrange("p t v u -> p (t v u)"),
+            )
+            acc = psum_h.tile([P, T_RUN, O], F32, tag="acc")
+            for i in range(T_RUN):
+                t = T_RUN * run + i
+                nc.tensor.matmul_mx(
+                    out=acc[:, i, :],
+                    lhsT=chan_codes[:, t, :].bitcast(FP8X4),
+                    lhsT_scale=chan_scales[:, t, :],
+                    rhs=w_codes[:, 0, :].bitcast(FP8X4),
+                    rhs_scale=w_scales[:, 0, :],
+                    start=True,
+                    stop=False,
+                )
+                nc.tensor.matmul_mx(
+                    out=acc[:, i, :],
+                    lhsT=tx1_codes[:, i, :].bitcast(FP8X4),
+                    lhsT_scale=tx1_scales[:, i, :],
+                    rhs=w_codes[:, 1, :].bitcast(FP8X4),
+                    rhs_scale=w_scales[:, 1, :],
+                    start=False,
+                    stop=True,
+                )
+            result = res_pool.tile([P, T_RUN, O], F32)
+            if b == 0:
+                nc.vector.tensor_copy(out=result[:], in_=acc[:])
+            else:
+                nc.scalar.copy(out=result[:], in_=acc[:])
+            nc.sync.dma_start(
+                out=out[b, T_RUN * run : T_RUN * (run + 1), nodes, :].rearrange("t n o -> n t o"),
+                in_=result[:],
+            )
+
+        for u in range(PACK):
+            raw_n = load_node_unit(0, u)
+            for run in range(RUNS):
+                quantise_node_unit(raw_n, 0, u, run)
+        chunk = load_channel_chunk(0, 0)
+        for run in range(RUNS):
+            quantise_channel_chunk(chunk, run)
+        for b in range(B):
+            for k in range(QUARTERS):
+                following = b * QUARTERS + k + 1
+                next_chunk = None
+                if following < B * QUARTERS:
+                    next_chunk = load_channel_chunk(following // QUARTERS, following % QUARTERS)
+                if b + 1 < B:
+                    raw_n = load_node_unit(b + 1, k)
+                for run in range(RUNS):
+                    if next_chunk is not None:
+                        quantise_channel_chunk(next_chunk, run)
+                    if b + 1 < B:
+                        quantise_node_unit(raw_n, b + 1, k, run)
+                    convolve(b, k, run, chunk[1], chunk[2])
+                chunk = next_chunk

@@ -34,30 +34,11 @@ def tile_dynamicgraphspatialconv_pa_t_kernel(
         chan_pool = ctx.enter_context(tc.tile_pool(name="chan", bufs=3))
         tx_pool = ctx.enter_context(tc.tile_pool(name="tx", bufs=2))
         res_pool = ctx.enter_context(tc.tile_pool(name="res", bufs=3))
-        psum_t = ctx.enter_context(tc.psum_pool(name="psum_t", bufs=2))
-        psum_tx = ctx.enter_context(tc.psum_pool(name="psum_tx", bufs=4))
+        banks = ctx.enter_context(tc.psum_pool(name="banks", bufs=6))
         psum_h = ctx.enter_context(tc.psum_pool(name="psum_h", bufs=2))
 
-        ident_bf16 = keep.tile([P, P], BF16)
-        make_identity(nc, ident_bf16[:])
         ident_f32 = keep.tile([P, P], F32)
         make_identity(nc, ident_f32[:])
-
-        w_codes = keep.tile([P, 2, PACK * O], U8, align_bytes=64)
-        w_scales = keep.tile([P, 2, O], U8, align_bytes=64)
-        nc.vector.memset(w_scales[:].rearrange("p w o -> p (w o)").bitcast(I32), 0)
-        for w, (words, scales) in enumerate(
-            ((w_cheb0_words, w_cheb0_scales), (w_cheb1_words, w_cheb1_scales))
-        ):
-            nc.sync.dma_start(
-                out=w_codes[:, w, :].bitcast(I32),
-                in_=words[0].rearrange("p o j -> p (o j)").bitcast(I32),
-            )
-            for quadrant in range(4):
-                nc.sync.dma_start(
-                    out=w_scales[32 * quadrant : 32 * quadrant + 4, w, :].bitcast(I32),
-                    in_=scales[0, 4 * quadrant : 4 * quadrant + 4, :].bitcast(I32),
-                )
 
         adj_sb = graph.tile([P, QUARTERS, N], BF16)
         nc.sync.dma_start(out=adj_sb[:], in_=adj_param.rearrange("(k p) v -> p k v", p=P))
@@ -77,7 +58,7 @@ def tile_dynamicgraphspatialconv_pa_t_kernel(
         sym = graph.tile([P, QUARTERS, N], F32)
         row_sum = graph.tile([P, QUARTERS], F32)
         for k in range(QUARTERS):
-            sig_t = psum_tx.tile([P, QUARTERS, P], F32, tag="bank")
+            sig_t = banks.tile([P, QUARTERS, P], F32, tag="bank")
             for kv in range(QUARTERS):
                 nc.tensor.transpose(sig_t[:, kv, :], sig[:, kv, k * P : (k + 1) * P], ident_f32[:])
             nc.vector.scalar_tensor_tensor(
@@ -132,29 +113,30 @@ def tile_dynamicgraphspatialconv_pa_t_kernel(
                 node_scales[(b, u)] = keep.tile([P, T, P], U8, name="node_scales_%d_%d" % (b, u), align_bytes=64)
 
         def load_node_unit(b, u):
-            raw_n = raw_pool.tile([P, QUARTERS, P, T], BF16)
-            source = x[b].rearrange("(a ml u) (j n) t -> u a ml j (n t)", a=QUARTERS, u=PACK, j=QUARTERS)
-            for a in range(QUARTERS):
-                nc.sync.dma_start(out=raw_n[:, a, :, :].rearrange("p n t -> p (n t)"), in_=source[u, a])
+            raw_n = raw_pool.tile([P, N, T], BF16)
+            source = x[b].rearrange("(m u) n t -> u m (n t)", u=PACK)
+            nc.sync.dma_start(out=raw_n[:].rearrange("m n t -> m (n t)"), in_=source[u])
             return raw_n
 
-        def quantise_node_unit(raw_n, b, u, run):
-            grouped_n = stage.tile([P, T_RUN, PACK * P], BF16, align_bytes=64)
+        def quantise_node_unit(raw_n, b, u, run, vector_helps):
+            time_pairs = raw_n[:].rearrange("m n t -> m (n t)").bitcast(F32)
+            time_pairs = time_pairs.rearrange("m (k n w) -> m k n w", k=QUARTERS, w=T // 2)
+            grouped_n = stage.tile([P, T_RUN, P, PACK], BF16, align_bytes=64)
             for half in range(2):
-                turned = psum_t.tile([P, 2, QUARTERS, P], BF16)
-                for i in range(2):
-                    t = T_RUN * run + 2 * half + i
-                    for a in range(QUARTERS):
-                        nc.tensor.transpose(turned[:, i, a, :], raw_n[:, a, :, t], ident_bf16[:])
-                nc.scalar.copy(
-                    out=grouped_n[:, 2 * half : 2 * half + 2, :],
-                    in_=turned[:].rearrange("p i a m -> p i (a m)"),
-                )
+                turned = banks.tile([P, QUARTERS, P], F32, tag="bank")
+                for k in range(QUARTERS):
+                    nc.tensor.transpose(turned[:, k, :], time_pairs[:, k, :, 2 * run + half], ident_f32[:])
+                single_times = turned[:].rearrange("p k m -> p (k m)").bitcast(BF16)
+                single_times = single_times.rearrange("p (k m e) -> p e m k", k=QUARTERS, e=2)
+                if vector_helps and half == 1:
+                    nc.vector.tensor_copy(out=grouped_n[:, 2 * half : 2 * half + 2, :, :], in_=single_times)
+                else:
+                    nc.scalar.copy(out=grouped_n[:, 2 * half : 2 * half + 2, :, :], in_=single_times)
             times = slice(T_RUN * run, T_RUN * (run + 1))
             nc.vector.quantize_mx(
                 out=node_codes[(b, u)][:, times, :].rearrange("p t m -> p (t m)").bitcast(FP8X4),
                 scales=node_scales[(b, u)][:, times, :].rearrange("p t m -> p (t m)"),
-                in_=grouped_n[:].rearrange("p t m -> p (t m)"),
+                in_=grouped_n[:].rearrange("p t m k -> p (t m k)"),
             )
 
         def load_channel_chunk(b, k):
@@ -184,7 +166,7 @@ def tile_dynamicgraphspatialconv_pa_t_kernel(
             grouped_x = stage.tile([P, T_RUN, P, PACK], BF16, align_bytes=64)
             for i in range(T_RUN):
                 t = T_RUN * run + i
-                tx1_bank = psum_tx.tile([P, PACK, P], F32, tag="bank")
+                tx1_bank = banks.tile([P, PACK, P], F32, tag="bank")
                 for u in range(PACK):
                     nc.tensor.matmul_mx(
                         out=tx1_bank[:, u, :],
@@ -237,10 +219,27 @@ def tile_dynamicgraphspatialconv_pa_t_kernel(
         for u in range(PACK):
             raw_n = load_node_unit(0, u)
             for run in range(RUNS):
-                quantise_node_unit(raw_n, 0, u, run)
+                quantise_node_unit(raw_n, 0, u, run, True)
         chunk = load_channel_chunk(0, 0)
         for run in range(RUNS):
             quantise_channel_chunk(chunk, run)
+
+        w_codes = keep.tile([P, 2, PACK * O], U8, align_bytes=64)
+        w_scales = keep.tile([P, 2, O], U8, align_bytes=64)
+        nc.vector.memset(w_scales[:].rearrange("p w o -> p (w o)").bitcast(I32), 0)
+        for w, (words, scales) in enumerate(
+            ((w_cheb0_words, w_cheb0_scales), (w_cheb1_words, w_cheb1_scales))
+        ):
+            nc.sync.dma_start(
+                out=w_codes[:, w, :].bitcast(I32),
+                in_=words[0].rearrange("p o j -> p (o j)").bitcast(I32),
+            )
+            for quadrant in range(4):
+                nc.sync.dma_start(
+                    out=w_scales[32 * quadrant : 32 * quadrant + 4, w, :].bitcast(I32),
+                    in_=scales[0, 4 * quadrant : 4 * quadrant + 4, :].bitcast(I32),
+                )
+
         for b in range(B):
             for k in range(QUARTERS):
                 following = b * QUARTERS + k + 1
@@ -253,6 +252,6 @@ def tile_dynamicgraphspatialconv_pa_t_kernel(
                     if next_chunk is not None:
                         quantise_channel_chunk(next_chunk, run)
                     if b + 1 < B:
-                        quantise_node_unit(raw_n, b + 1, k, run)
+                        quantise_node_unit(raw_n, b + 1, k, run, False)
                     convolve(b, k, run, chunk[1], chunk[2])
                 chunk = next_chunk

@@ -113,12 +113,12 @@ def tile_dynamicgraphspatialconv_pa_t_kernel(
                 node_scales[(b, u)] = keep.tile([P, T, P], U8, name="node_scales_%d_%d" % (b, u), align_bytes=64)
 
         def load_node_unit(b, u):
-            raw_n = raw_pool.tile([P, N, T], BF16)
+            raw_n = raw_pool.tile([P, N, T], BF16, bufs=3)
             source = x[b].rearrange("(m u) n t -> u m (n t)", u=PACK)
             nc.sync.dma_start(out=raw_n[:].rearrange("m n t -> m (n t)"), in_=source[u])
             return raw_n
 
-        def quantise_node_unit(raw_n, b, u, run, vector_helps):
+        def quantise_node_unit(raw_n, b, u, run):
             time_pairs = raw_n[:].rearrange("m n t -> m (n t)").bitcast(F32)
             time_pairs = time_pairs.rearrange("m (k n w) -> m k n w", k=QUARTERS, w=T // 2)
             grouped_n = stage.tile([P, T_RUN, P, PACK], BF16, align_bytes=64)
@@ -128,7 +128,7 @@ def tile_dynamicgraphspatialconv_pa_t_kernel(
                     nc.tensor.transpose(turned[:, k, :], time_pairs[:, k, :, 2 * run + half], ident_f32[:])
                 single_times = turned[:].rearrange("p k m -> p (k m)").bitcast(BF16)
                 single_times = single_times.rearrange("p (k m e) -> p e m k", k=QUARTERS, e=2)
-                if vector_helps and half == 1:
+                if run == RUNS - 1:
                     nc.vector.tensor_copy(out=grouped_n[:, 2 * half : 2 * half + 2, :, :], in_=single_times)
                 else:
                     nc.scalar.copy(out=grouped_n[:, 2 * half : 2 * half + 2, :, :], in_=single_times)
@@ -207,22 +207,20 @@ def tile_dynamicgraphspatialconv_pa_t_kernel(
                     stop=True,
                 )
             result = res_pool.tile([P, T_RUN, O], F32)
-            if b == 0:
-                nc.vector.tensor_copy(out=result[:], in_=acc[:])
-            else:
+            if (k * RUNS + run) % 2 == 0:
                 nc.scalar.copy(out=result[:], in_=acc[:])
+            else:
+                nc.vector.tensor_copy(out=result[:], in_=acc[:])
             nc.sync.dma_start(
                 out=out[b, T_RUN * run : T_RUN * (run + 1), nodes, :].rearrange("t n o -> n t o"),
                 in_=result[:],
             )
 
-        for u in range(PACK):
-            raw_n = load_node_unit(0, u)
-            for run in range(RUNS):
-                quantise_node_unit(raw_n, 0, u, run, True)
-        chunk = load_channel_chunk(0, 0)
-        for run in range(RUNS):
-            quantise_channel_chunk(chunk, run)
+        for b in range(B):
+            for u in range(PACK):
+                raw_n = load_node_unit(b, u)
+                for run in range(RUNS):
+                    quantise_node_unit(raw_n, b, u, run)
 
         w_codes = keep.tile([P, 2, PACK * O], U8, align_bytes=64)
         w_scales = keep.tile([P, 2, O], U8, align_bytes=64)
@@ -240,18 +238,17 @@ def tile_dynamicgraphspatialconv_pa_t_kernel(
                     in_=scales[0, 4 * quadrant : 4 * quadrant + 4, :].bitcast(I32),
                 )
 
+        chunk = load_channel_chunk(0, 0)
+        for run in range(RUNS):
+            quantise_channel_chunk(chunk, run)
         for b in range(B):
             for k in range(QUARTERS):
                 following = b * QUARTERS + k + 1
                 next_chunk = None
                 if following < B * QUARTERS:
                     next_chunk = load_channel_chunk(following // QUARTERS, following % QUARTERS)
-                if b + 1 < B:
-                    raw_n = load_node_unit(b + 1, k)
                 for run in range(RUNS):
                     if next_chunk is not None:
                         quantise_channel_chunk(next_chunk, run)
-                    if b + 1 < B:
-                        quantise_node_unit(raw_n, b + 1, k, run, False)
                     convolve(b, k, run, chunk[1], chunk[2])
                 chunk = next_chunk

@@ -128,7 +128,7 @@ def tile_dynamicgraphspatialconv_pa_t_kernel(
                     nc.tensor.transpose(turned[:, k, :], time_pairs[:, k, :, 2 * run + half], ident_f32[:])
                 single_times = turned[:].rearrange("p k m -> p (k m)").bitcast(BF16)
                 single_times = single_times.rearrange("p (k m e) -> p e m k", k=QUARTERS, e=2)
-                if run == RUNS - 1:
+                if run == 0:
                     nc.vector.tensor_copy(out=grouped_n[:, 2 * half : 2 * half + 2, :, :], in_=single_times)
                 else:
                     nc.scalar.copy(out=grouped_n[:, 2 * half : 2 * half + 2, :, :], in_=single_times)
@@ -161,9 +161,9 @@ def tile_dynamicgraphspatialconv_pa_t_kernel(
                 in_=grouped_c[:].rearrange("p t n j -> p (t n j)"),
             )
 
-        def convolve(b, k, run, chan_codes, chan_scales):
+        def convolve(b, k, run, chan_codes, chan_scales, vector_is_free):
             nodes = slice(k * P, (k + 1) * P)
-            grouped_x = stage.tile([P, T_RUN, P, PACK], BF16, align_bytes=64)
+            grouped_x = stage.tile([P, T_RUN, P, PACK], BF16, align_bytes=64, bufs=4)
             for i in range(T_RUN):
                 t = T_RUN * run + i
                 tx1_bank = banks.tile([P, PACK, P], F32, tag="bank")
@@ -177,7 +177,10 @@ def tile_dynamicgraphspatialconv_pa_t_kernel(
                         start=True,
                         stop=True,
                     )
-                nc.scalar.copy(out=grouped_x[:, i, :, :], in_=tx1_bank[:].rearrange("p u v -> p v u"))
+                if vector_is_free and i % 2 == 1:
+                    nc.vector.tensor_copy(out=grouped_x[:, i, :, :], in_=tx1_bank[:].rearrange("p u v -> p v u"))
+                else:
+                    nc.scalar.copy(out=grouped_x[:, i, :, :], in_=tx1_bank[:].rearrange("p u v -> p v u"))
             tx1_codes = tx_pool.tile([P, T_RUN, P], U32, align_bytes=64)
             tx1_scales = tx_pool.tile([P, T_RUN, P], U8, align_bytes=64)
             nc.vector.quantize_mx(
@@ -207,10 +210,7 @@ def tile_dynamicgraphspatialconv_pa_t_kernel(
                     stop=True,
                 )
             result = res_pool.tile([P, T_RUN, O], F32)
-            if (k * RUNS + run) % 2 == 0:
-                nc.scalar.copy(out=result[:], in_=acc[:])
-            else:
-                nc.vector.tensor_copy(out=result[:], in_=acc[:])
+            nc.scalar.copy(out=result[:], in_=acc[:])
             nc.sync.dma_start(
                 out=out[b, T_RUN * run : T_RUN * (run + 1), nodes, :].rearrange("t n o -> n t o"),
                 in_=result[:],
@@ -250,5 +250,5 @@ def tile_dynamicgraphspatialconv_pa_t_kernel(
                 for run in range(RUNS):
                     if next_chunk is not None:
                         quantise_channel_chunk(next_chunk, run)
-                    convolve(b, k, run, chunk[1], chunk[2])
+                    convolve(b, k, run, chunk[1], chunk[2], next_chunk is None)
                 chunk = next_chunk

@@ -18,6 +18,8 @@ B, C, N, T, O = 2, 512, 512, 12, 128
 QUARTERS = N // P
 T_RUN = 4
 RUNS = T // T_RUN
+GROUPS = B * RUNS
+GROUPED = 12
 
 FLOPS = 2 * B * T * (N * N * C + 2 * N * C * O)
 
@@ -29,172 +31,129 @@ def tile_dynamicgraphspatialconv_pa_t_kernel(
     with ExitStack() as ctx:
         keep = ctx.enter_context(tc.tile_pool(name="keep", bufs=1))
         graph = ctx.enter_context(tc.tile_pool(name="graph", bufs=1))
-        raw_pool = ctx.enter_context(tc.tile_pool(name="raw", bufs=2))
+        raw_pool = ctx.enter_context(tc.tile_pool(name="raw", bufs=6))
         stage = ctx.enter_context(tc.tile_pool(name="stage", bufs=3))
-        chan_pool = ctx.enter_context(tc.tile_pool(name="chan", bufs=3))
-        tx_pool = ctx.enter_context(tc.tile_pool(name="tx", bufs=2))
+        code_pool = ctx.enter_context(tc.tile_pool(name="codes", bufs=6))
         res_pool = ctx.enter_context(tc.tile_pool(name="res", bufs=3))
-        banks = ctx.enter_context(tc.psum_pool(name="banks", bufs=6))
-        psum_h = ctx.enter_context(tc.psum_pool(name="psum_h", bufs=2))
+        psum = ctx.enter_context(tc.psum_pool(name="psum", bufs=2))
 
         ident_f32 = keep.tile([P, P], F32)
         make_identity(nc, ident_f32[:])
+        ctx.enter_context(tc.manual_schedule())
 
-        adj_sb = graph.tile([P, QUARTERS, N], BF16)
-        nc.sync.dma_start(out=adj_sb[:], in_=adj_param.rearrange("(k p) v -> p k v", p=P))
-        sig = graph.tile([P, QUARTERS, N], F32)
-        nc.scalar.activation(out=sig[:], in_=adj_sb[:], func=ACT.Sigmoid)
-        for k in range(QUARTERS):
-            diagonal_block = sig[:, k, k * P : (k + 1) * P]
-            nc.gpsimd.affine_select(
-                out=diagonal_block,
-                in_=diagonal_block,
-                compare_op=ALU.not_equal,
-                fill=0.0,
-                base=0,
-                pattern=[[-1, P]],
-                channel_multiplier=1,
-            )
-        sym = graph.tile([P, QUARTERS, N], F32)
-        row_sum = graph.tile([P, QUARTERS], F32)
-        for k in range(QUARTERS):
-            sig_t = banks.tile([P, QUARTERS, P], F32, tag="bank")
-            for kv in range(QUARTERS):
-                nc.tensor.transpose(sig_t[:, kv, :], sig[:, kv, k * P : (k + 1) * P], ident_f32[:])
-            nc.vector.scalar_tensor_tensor(
-                out=sym[:, k, :],
-                in0=sig[:, k, :],
-                scalar=1.0,
-                in1=sig_t[:].rearrange("p k v -> p (k v)"),
-                op0=ALU.mult,
-                op1=ALU.add,
-                accum_out=row_sum[:, k : k + 1],
-            )
-        root = graph.tile([P, QUARTERS], F32)
-        nc.scalar.activation(out=root[:], in_=row_sum[:], func=ACT.Sqrt, scale=0.5)
-        dis = graph.tile([P, QUARTERS], F32)
-        nc.vector.reciprocal(out=dis[:], in_=root[:])
-        minus_half_dis = graph.tile([P, QUARTERS], F32)
-        nc.vector.tensor_scalar_mul(out=minus_half_dis[:], in0=dis[:], scalar1=-0.5)
-        dis_row = psum_h.tile([P, QUARTERS, P], F32, tag="acc")
-        for k in range(QUARTERS):
-            nc.tensor.matmul(
-                out=dis_row[:, k, :],
-                lhsT=dis[:, k : k + 1].to_broadcast([P, P]),
-                rhs=ident_f32[:],
-                start=True,
-                stop=True,
-            )
-        s_rows = graph.tile([P, QUARTERS, N], BF16)
-        for k in range(QUARTERS):
-            nc.vector.scalar_tensor_tensor(
-                out=s_rows[:, k, :],
-                in0=sym[:, k, :],
-                scalar=minus_half_dis[:, k : k + 1],
-                in1=dis_row[:].rearrange("p k v -> p (k v)"),
-                op0=ALU.mult,
-                op1=ALU.mult,
-            )
-        s_grouped = graph.tile([P, N, PACK], BF16, align_bytes=64)
-        nc.vector.tensor_copy(out=s_grouped[:], in_=s_rows[:].rearrange("p k v -> p v k"))
-        s_codes = keep.tile([P, N], U32, align_bytes=64)
-        s_scales = keep.tile([P, N], U8, align_bytes=64)
-        nc.vector.quantize_mx(
-            out=s_codes[:].bitcast(FP8X4),
-            scales=s_scales[:],
-            in_=s_grouped[:].rearrange("p v k -> p (v k)"),
-        )
+        def copy_on(engine, dst, src):
+            if engine == "vector":
+                nc.vector.tensor_copy(out=dst, in_=src)
+            else:
+                nc.scalar.copy(out=dst, in_=src)
 
-        node_codes = {}
-        node_scales = {}
-        for b in range(B):
-            for u in range(PACK):
-                node_codes[(b, u)] = keep.tile([P, T, P], U32, name="node_codes_%d_%d" % (b, u), align_bytes=64)
-                node_scales[(b, u)] = keep.tile([P, T, P], U8, name="node_scales_%d_%d" % (b, u), align_bytes=64)
+        raw = {}
 
-        def load_node_unit(b, u):
-            raw_n = raw_pool.tile([P, N, T], BF16, bufs=3)
-            source = x[b].rearrange("(m u) n t -> u m (n t)", u=PACK)
-            nc.sync.dma_start(out=raw_n[:].rearrange("m n t -> m (n t)"), in_=source[u])
-            return raw_n
-
-        def quantise_node_unit(raw_n, b, u, run):
-            time_pairs = raw_n[:].rearrange("m n t -> m (n t)").bitcast(F32)
-            time_pairs = time_pairs.rearrange("m (k n w) -> m k n w", k=QUARTERS, w=T // 2)
-            grouped_n = stage.tile([P, T_RUN, P, PACK], BF16, align_bytes=64)
-            for half in range(2):
-                turned = banks.tile([P, QUARTERS, P], F32, tag="bank")
-                for k in range(QUARTERS):
-                    nc.tensor.transpose(turned[:, k, :], time_pairs[:, k, :, 2 * run + half], ident_f32[:])
-                single_times = turned[:].rearrange("p k m -> p (k m)").bitcast(BF16)
-                single_times = single_times.rearrange("p (k m e) -> p e m k", k=QUARTERS, e=2)
-                if run == 0:
-                    nc.vector.tensor_copy(out=grouped_n[:, 2 * half : 2 * half + 2, :, :], in_=single_times)
-                else:
-                    nc.scalar.copy(out=grouped_n[:, 2 * half : 2 * half + 2, :, :], in_=single_times)
-            times = slice(T_RUN * run, T_RUN * (run + 1))
-            nc.vector.quantize_mx(
-                out=node_codes[(b, u)][:, times, :].rearrange("p t m -> p (t m)").bitcast(FP8X4),
-                scales=node_scales[(b, u)][:, times, :].rearrange("p t m -> p (t m)"),
-                in_=grouped_n[:].rearrange("p t m k -> p (t m k)"),
-            )
-
-        def load_channel_chunk(b, k):
+        def load_quarter(b, k, pieces=1):
             raw_c = raw_pool.tile([P, PACK, P, T], BF16)
-            source = x[b].rearrange("(p j) (k n) t -> k p j (n t)", j=PACK, k=QUARTERS)
-            nc.sync.dma_start(out=raw_c[:].rearrange("p j n t -> p j (n t)"), in_=source[k])
-            chan_codes = chan_pool.tile([P, T, P], U32, align_bytes=64)
-            chan_scales = chan_pool.tile([P, T, P], U8, align_bytes=64)
-            return raw_c, chan_codes, chan_scales
+            source = x[b].rearrange("(p j) (k n) t -> k p j n t", j=PACK, k=QUARTERS)
+            raw[(b, k)] = raw_c
+            for n in range(0, P, P // pieces):
+                nodes = slice(n, n + P // pieces)
+                nc.sync.dma_start(
+                    out=raw_c[:, :, nodes, :].rearrange("p j n t -> p j (n t)"),
+                    in_=source[k][:, :, nodes, :].rearrange("p j n t -> p j (n t)"),
+                )
 
-        def quantise_channel_chunk(chunk, run):
-            raw_c, chan_codes, chan_scales = chunk
-            times = slice(T_RUN * run, T_RUN * (run + 1))
-            grouped_c = stage.tile([P, T_RUN, P, PACK], BF16, align_bytes=64)
-            nc.vector.tensor_copy(
-                out=grouped_c[:].rearrange("p t n j -> p n j t"),
-                in_=raw_c[:, :, :, times].rearrange("p j n t -> p n j t"),
+        grouped = {}
+        chan = {}
+
+        def group_channels(g, k, engine, nodes=slice(0, P)):
+            first = T_RUN * (g % RUNS)
+            if nodes.start == 0:
+                grouped_c = stage.tile([P, T_RUN, P, PACK], BF16, align_bytes=64, bufs=GROUPED)
+                grouped[(g, k)] = grouped_c
+            copy_on(
+                engine,
+                grouped[(g, k)][:, :, nodes, :].rearrange("p t n j -> p n j t"),
+                raw[(g // RUNS, k)][:, :, nodes, first : first + T_RUN].rearrange("p j n t -> p n j t"),
             )
+
+        def quantise_channels(g, k):
+            chan_codes = code_pool.tile([P, T_RUN, P], U32, align_bytes=64, bufs=11)
+            chan_scales = code_pool.tile([P, T_RUN, P], U8, align_bytes=64, bufs=11)
             nc.vector.quantize_mx(
-                out=chan_codes[:, times, :].rearrange("p t n -> p (t n)").bitcast(FP8X4),
-                scales=chan_scales[:, times, :].rearrange("p t n -> p (t n)"),
-                in_=grouped_c[:].rearrange("p t n j -> p (t n j)"),
+                out=chan_codes[:].rearrange("p t n -> p (t n)").bitcast(FP8X4),
+                scales=chan_scales[:].rearrange("p t n -> p (t n)"),
+                in_=grouped[(g, k)][:].rearrange("p t n j -> p (t n j)"),
             )
+            chan[(g, k)] = (chan_codes, chan_scales)
 
-        def convolve(b, k, run, chan_codes, chan_scales, vector_is_free):
+        node = {}
+
+        def turn_nodes(g, i, h, tag, bufs):
+            turned = psum.tile([P, QUARTERS, P], F32, tag=tag, bufs=bufs)
+            for k in range(QUARTERS):
+                words = grouped[(g, k)][:].rearrange("p t n j -> p (t n j)").bitcast(F32)
+                words = words.rearrange("p (t n h) -> p t n h", t=T_RUN, h=2)
+                nc.tensor.transpose(turned[:, k, :], words[:, i, :, h], ident_f32[:])
+            return turned
+
+        def empty_turned(turned, grouped_n, h, engine):
+            single_channels = turned[:].rearrange("p k m -> p (k m)").bitcast(BF16)
+            single_channels = single_channels.rearrange("p (k m e) -> p e m k", k=QUARTERS, e=2)
+            copy_on(engine, grouped_n[:, 2 * h : 2 * h + 2, :, :], single_channels)
+
+        def new_grouped_n():
+            grouped_n = stage.tile([P, PACK, P, QUARTERS], BF16, align_bytes=64)
+            return grouped_n
+
+        def quantise_nodes(g, i, grouped_n):
+            node_codes = code_pool.tile([P, PACK, P], U32, align_bytes=64)
+            node_scales = code_pool.tile([P, PACK, P], U8, align_bytes=64)
+            nc.vector.quantize_mx(
+                out=node_codes[:].rearrange("p u m -> p (u m)").bitcast(FP8X4),
+                scales=node_scales[:].rearrange("p u m -> p (u m)"),
+                in_=grouped_n[:].rearrange("p u m k -> p (u m k)"),
+            )
+            node[(g, i)] = (node_codes, node_scales)
+
+        def make_tx1(g, k, vector_banks):
             nodes = slice(k * P, (k + 1) * P)
-            grouped_x = stage.tile([P, T_RUN, P, PACK], BF16, align_bytes=64, bufs=4)
+            grouped_x = stage.tile([P, T_RUN, P, PACK], BF16, align_bytes=64)
             for i in range(T_RUN):
-                t = T_RUN * run + i
-                tx1_bank = banks.tile([P, PACK, P], F32, tag="bank")
+                tx1_bank = psum.tile([P, PACK, P], F32, tag="tx1", bufs=4)
+                node_codes, node_scales = node[(g, i)]
                 for u in range(PACK):
                     nc.tensor.matmul_mx(
                         out=tx1_bank[:, u, :],
-                        lhsT=node_codes[(b, u)][:, t, :].bitcast(FP8X4),
-                        lhsT_scale=node_scales[(b, u)][:, t, :],
+                        lhsT=node_codes[:, u, :].bitcast(FP8X4),
+                        lhsT_scale=node_scales[:, u, :],
                         rhs=s_codes[:, nodes].bitcast(FP8X4),
                         rhs_scale=s_scales[:, nodes],
                         start=True,
                         stop=True,
                     )
-                if vector_is_free and i % 2 == 1:
-                    nc.vector.tensor_copy(out=grouped_x[:, i, :, :], in_=tx1_bank[:].rearrange("p u v -> p v u"))
-                else:
-                    nc.scalar.copy(out=grouped_x[:, i, :, :], in_=tx1_bank[:].rearrange("p u v -> p v u"))
-            tx1_codes = tx_pool.tile([P, T_RUN, P], U32, align_bytes=64)
-            tx1_scales = tx_pool.tile([P, T_RUN, P], U8, align_bytes=64)
+                copy_on(
+                    "vector" if i in vector_banks else "scalar",
+                    grouped_x[:, i, :, :],
+                    tx1_bank[:].rearrange("p u v -> p v u"),
+                )
+            return grouped_x
+
+        def quantise_tx1(grouped_x):
+            tx1_codes = stage.tile([P, T_RUN, P], U32, align_bytes=64)
+            tx1_scales = stage.tile([P, T_RUN, P], U8, align_bytes=64)
             nc.vector.quantize_mx(
                 out=tx1_codes[:].rearrange("p t v -> p (t v)").bitcast(FP8X4),
                 scales=tx1_scales[:].rearrange("p t v -> p (t v)"),
                 in_=grouped_x[:].rearrange("p t v u -> p (t v u)"),
             )
-            acc = psum_h.tile([P, T_RUN, O], F32, tag="acc")
+            return tx1_codes, tx1_scales
+
+        def add_orders(g, k, tx1_codes, tx1_scales):
+            chan_codes, chan_scales = chan[(g, k)]
+            acc = psum.tile([P, T_RUN, O], F32, tag="acc", bufs=2)
             for i in range(T_RUN):
-                t = T_RUN * run + i
                 nc.tensor.matmul_mx(
                     out=acc[:, i, :],
-                    lhsT=chan_codes[:, t, :].bitcast(FP8X4),
-                    lhsT_scale=chan_scales[:, t, :],
+                    lhsT=chan_codes[:, i, :].bitcast(FP8X4),
+                    lhsT_scale=chan_scales[:, i, :],
                     rhs=w_codes[:, 0, :].bitcast(FP8X4),
                     rhs_scale=w_scales[:, 0, :],
                     start=True,
@@ -209,22 +168,29 @@ def tile_dynamicgraphspatialconv_pa_t_kernel(
                     start=False,
                     stop=True,
                 )
+            return acc
+
+        def store_result(g, k, acc):
             result = res_pool.tile([P, T_RUN, O], F32)
             nc.scalar.copy(out=result[:], in_=acc[:])
+            first = T_RUN * (g % RUNS)
             nc.sync.dma_start(
-                out=out[b, T_RUN * run : T_RUN * (run + 1), nodes, :].rearrange("t n o -> n t o"),
+                out=out[g // RUNS, first : first + T_RUN, k * P : (k + 1) * P, :].rearrange("t n o -> n t o"),
                 in_=result[:],
             )
 
-        for b in range(B):
-            for u in range(PACK):
-                raw_n = load_node_unit(b, u)
-                for run in range(RUNS):
-                    quantise_node_unit(raw_n, b, u, run)
+        first_half, second_half = slice(0, P // 2), slice(P // 2, P)
+        load_quarter(0, 0, 2)
+        adj_sb = graph.tile([P, QUARTERS, N], BF16)
+        nc.sync.dma_start(out=adj_sb[:], in_=adj_param.rearrange("(k p) v -> p k v", p=P))
+        for k in range(1, QUARTERS):
+            load_quarter(0, k)
 
         w_codes = keep.tile([P, 2, PACK * O], U8, align_bytes=64)
         w_scales = keep.tile([P, 2, O], U8, align_bytes=64)
-        nc.vector.memset(w_scales[:].rearrange("p w o -> p (w o)").bitcast(I32), 0)
+        nc.gpsimd.memset(w_scales[:].rearrange("p w o -> p (w o)").bitcast(I32), 0)
+        minus_half = graph.tile([P, QUARTERS], F32)
+        nc.gpsimd.memset(minus_half[:], -0.5)
         for w, (words, scales) in enumerate(
             ((w_cheb0_words, w_cheb0_scales), (w_cheb1_words, w_cheb1_scales))
         ):
@@ -237,18 +203,151 @@ def tile_dynamicgraphspatialconv_pa_t_kernel(
                     out=w_scales[32 * quadrant : 32 * quadrant + 4, w, :].bitcast(I32),
                     in_=scales[0, 4 * quadrant : 4 * quadrant + 4, :].bitcast(I32),
                 )
+        load_quarter(1, 0)
+        load_quarter(1, 1)
 
-        chunk = load_channel_chunk(0, 0)
-        for run in range(RUNS):
-            quantise_channel_chunk(chunk, run)
-        for b in range(B):
+        sig = graph.tile([P, QUARTERS, N], F32)
+        sym = graph.tile([P, QUARTERS, N], F32)
+        row_sum = graph.tile([P, QUARTERS], F32)
+        dis = graph.tile([P, QUARTERS], F32)
+        minus_dis = graph.tile([P, QUARTERS], F32)
+        s_rows = graph.tile([P, QUARTERS, N], BF16)
+        s_grouped = graph.tile([P, N, PACK], BF16, align_bytes=64)
+        s_codes = keep.tile([P, N], U32, align_bytes=64)
+        s_scales = keep.tile([P, N], U8, align_bytes=64)
+
+        def sigmoids():
+            nc.scalar.activation(out=sig[:], in_=adj_sb[:], func=ACT.Sigmoid)
             for k in range(QUARTERS):
-                following = b * QUARTERS + k + 1
-                next_chunk = None
-                if following < B * QUARTERS:
-                    next_chunk = load_channel_chunk(following // QUARTERS, following % QUARTERS)
-                for run in range(RUNS):
-                    if next_chunk is not None:
-                        quantise_channel_chunk(next_chunk, run)
-                    convolve(b, k, run, chunk[1], chunk[2], next_chunk is None)
-                chunk = next_chunk
+                diagonal_block = sig[:, k, k * P : (k + 1) * P]
+                nc.gpsimd.affine_select(
+                    out=diagonal_block,
+                    in_=diagonal_block,
+                    compare_op=ALU.not_equal,
+                    fill=0.0,
+                    base=0,
+                    pattern=[[-1, P]],
+                    channel_multiplier=1,
+                )
+
+        def symmetrise():
+            for k in range(QUARTERS):
+                sig_t = psum.tile([P, QUARTERS, P], F32, tag="tx1", bufs=4)
+                for kv in range(QUARTERS):
+                    nc.tensor.transpose(sig_t[:, kv, :], sig[:, kv, k * P : (k + 1) * P], ident_f32[:])
+                nc.vector.scalar_tensor_tensor(
+                    out=sym[:, k, :],
+                    in0=sig[:, k, :],
+                    scalar=1.0,
+                    in1=sig_t[:].rearrange("p k v -> p (k v)"),
+                    op0=ALU.mult,
+                    op1=ALU.add,
+                    accum_out=row_sum[:, k : k + 1],
+                )
+
+        def spread_degrees():
+            nc.gpsimd.tensor_tensor(out=dis[:], in0=row_sum[:], in1=minus_half[:], op=ALU.pow)
+            nc.gpsimd.tensor_scalar_mul(out=minus_dis[:], in0=dis[:], scalar1=-1.0)
+            dis_row = psum.tile([P, QUARTERS, P], F32, tag="acc", bufs=2)
+            for k in range(QUARTERS):
+                nc.tensor.matmul(
+                    out=dis_row[:, k, :],
+                    lhsT=dis[:, k : k + 1].to_broadcast([P, P]),
+                    rhs=ident_f32[:],
+                    start=True,
+                    stop=True,
+                )
+            return dis_row
+
+        def normalise(dis_row):
+            for k in range(QUARTERS):
+                nc.vector.scalar_tensor_tensor(
+                    out=s_rows[:, k, :],
+                    in0=sym[:, k, :],
+                    scalar=minus_dis[:, k : k + 1],
+                    in1=dis_row[:].rearrange("p k v -> p (k v)"),
+                    op0=ALU.mult,
+                    op1=ALU.mult,
+                )
+
+        def group_s():
+            nc.vector.tensor_copy(out=s_grouped[:], in_=s_rows[:].rearrange("p k v -> p v k"))
+
+        def quantise_s():
+            nc.vector.quantize_mx(
+                out=s_codes[:].bitcast(FP8X4),
+                scales=s_scales[:],
+                in_=s_grouped[:].rearrange("p v k -> p (v k)"),
+            )
+
+        def turn(step, engines, tags=("tr", "tr")):
+            grouped_n = new_grouped_n()
+            for h in range(2):
+                turned = turn_nodes(step // T_RUN, step % T_RUN, h, tags[h], 2 if tags[h] == "tr" else 4)
+                empty_turned(turned, grouped_n, h, engines[h])
+            return grouped_n
+
+        for half in (first_half, second_half):
+            group_channels(0, 0, "vector", half)
+            group_channels(1, 0, "scalar", half)
+            if half is first_half:
+                sigmoids()
+            group_channels(2, 0, "vector", half)
+        symmetrise()
+        dis_row = spread_degrees()
+        group_channels(0, 1, "vector")
+        group_channels(1, 1, "scalar")
+        quantise_channels(0, 0)
+        quantise_channels(1, 0)
+        group_channels(0, 2, "vector")
+        group_channels(1, 2, "scalar")
+        group_channels(0, 3, "vector")
+        group_channels(1, 3, "scalar")
+        turned_0 = turn(0, ("scalar", "scalar"), ("tr", "tx1"))
+        normalise(dis_row)
+        group_s()
+        quantise_s()
+        turned_1 = turn(1, ("scalar", "scalar"), ("tr", "tx1"))
+        quantise_nodes(0, 0, turned_0)
+        turned_2 = turn(2, ("scalar", "scalar"), ("tr", "tx1"))
+        quantise_nodes(0, 1, turned_1)
+        turned_3 = turn(3, ("scalar", "vector"), ("tr", "tx1"))
+        quantise_nodes(0, 2, turned_2)
+        waiting_nodes = (0, 3, turned_3)
+
+        quantise_order = [(0, 1), (0, 2), (0, 3), (1, 1), (1, 2), (1, 3), (2, 0)]
+        waiting_tx1 = None
+        for step in range(-1, GROUPS * QUARTERS + 1):
+            g, k = divmod(step, QUARTERS)
+            laid, turning = step + 9, step + 5
+            lays, turns = 0 <= step and laid < GROUPS * QUARTERS, turning < GROUPS * QUARTERS
+            if lays:
+                vector_banks = ()
+            elif turns:
+                vector_banks = (3,)
+            else:
+                vector_banks = (1, 3)
+            tx1_words = None
+            if waiting_tx1 is not None:
+                tx1_words = quantise_tx1(waiting_tx1[2])
+            if lays:
+                group_channels(laid // QUARTERS, laid % QUARTERS, "vector")
+            grouped_x = None
+            if 0 <= step < GROUPS * QUARTERS:
+                grouped_x = make_tx1(g, k, vector_banks)
+            grouped_n = None
+            if turns:
+                grouped_n = turn(turning, ("scalar", "scalar") if lays and k == 3 else ("vector", "scalar"))
+            if tx1_words is not None:
+                acc = add_orders(waiting_tx1[0], waiting_tx1[1], *tx1_words)
+                store_result(waiting_tx1[0], waiting_tx1[1], acc)
+            waiting_tx1 = None if grouped_x is None else (g, k, grouped_x)
+            if waiting_nodes is not None:
+                quantise_nodes(*waiting_nodes)
+            waiting_nodes = None if grouped_n is None else (turning // T_RUN, turning % T_RUN, grouped_n)
+            if quantise_order:
+                quantise_channels(*quantise_order.pop(0))
+            if lays:
+                quantise_order.append((laid // QUARTERS, laid % QUARTERS))
+            if 0 <= step < 2:
+                load_quarter(1, step + 2)

@@ -19,7 +19,11 @@ QUARTERS = N // P
 T_RUN = 4
 RUNS = T // T_RUN
 GROUPS = B * RUNS
-GROUPED = 12
+BLOCKS = C * QUARTERS // P
+LOADED = 4
+BANKED = 8
+GROUPED = 9
+EMPTY_ORDER = (1, 0, 3, 2)
 
 FLOPS = 2 * B * T * (N * N * C + 2 * N * C * O)
 
@@ -31,7 +35,8 @@ def tile_dynamicgraphspatialconv_pa_t_kernel(
     with ExitStack() as ctx:
         keep = ctx.enter_context(tc.tile_pool(name="keep", bufs=1))
         graph = ctx.enter_context(tc.tile_pool(name="graph", bufs=1))
-        raw_pool = ctx.enter_context(tc.tile_pool(name="raw", bufs=6))
+        raw_pool = ctx.enter_context(tc.tile_pool(name="raw", bufs=5))
+        rows_pool = ctx.enter_context(tc.tile_pool(name="rows", bufs=BLOCKS // LOADED))
         stage = ctx.enter_context(tc.tile_pool(name="stage", bufs=3))
         code_pool = ctx.enter_context(tc.tile_pool(name="codes", bufs=6))
         res_pool = ctx.enter_context(tc.tile_pool(name="res", bufs=3))
@@ -39,6 +44,11 @@ def tile_dynamicgraphspatialconv_pa_t_kernel(
 
         ident_f32 = keep.tile([P, P], F32)
         make_identity(nc, ident_f32[:])
+        spread = keep.tile([P, P], BF16)
+        nc.gpsimd.tensor_copy(
+            out=spread[:].rearrange("p (u m k) -> p m u k", u=PACK, k=QUARTERS),
+            in_=ident_f32[:].rearrange("p (m u k) -> p m u k", u=PACK, k=QUARTERS),
+        )
         ctx.enter_context(tc.manual_schedule())
 
         def copy_on(engine, dst, src):
@@ -59,6 +69,17 @@ def tile_dynamicgraphspatialconv_pa_t_kernel(
                     out=raw_c[:, :, nodes, :].rearrange("p j n t -> p j (n t)"),
                     in_=source[k][:, :, nodes, :].rearrange("p j n t -> p j (n t)"),
                 )
+
+        rows = {}
+
+        def load_blocks(b, first):
+            rows_b = rows_pool.tile([P, LOADED, P, T], BF16, tag="rows")
+            source = x[b].rearrange("(a c) (k n) t -> (c k) a (n t)", a=BLOCKS, k=QUARTERS)
+            nc.sync.dma_start(
+                out=rows_b[:].rearrange("q a n t -> q a (n t)"), in_=source[:, first : first + LOADED, :]
+            )
+            for a in range(LOADED):
+                rows[(b, first + a)] = rows_b[:, a, :, :]
 
         grouped = {}
         chan = {}
@@ -99,8 +120,24 @@ def tile_dynamicgraphspatialconv_pa_t_kernel(
             single_channels = single_channels.rearrange("p (k m e) -> p e m k", k=QUARTERS, e=2)
             copy_on(engine, grouped_n[:, 2 * h : 2 * h + 2, :, :], single_channels)
 
+        def spread_rows(time, half, engine, grouped_n, tag, bufs):
+            turned = psum.tile([P, BANKED, P], BF16, tag=tag, bufs=bufs)
+            for a in range(BANKED):
+                nc.tensor.matmul(
+                    out=turned[:, a, :],
+                    lhsT=rows[(time // T, BANKED * half + a)][:, :, time % T],
+                    rhs=spread[:],
+                    start=True,
+                    stop=True,
+                )
+            copy_on(
+                engine,
+                grouped_n[:, :, half * P // 2 : (half + 1) * P // 2, :].rearrange("p u (a m) k -> p u a (m k)", a=BANKED),
+                turned[:].rearrange("p a (u w) -> p u a w", u=PACK),
+            )
+
         def new_grouped_n():
-            grouped_n = stage.tile([P, PACK, P, QUARTERS], BF16, align_bytes=64)
+            grouped_n = stage.tile([P, PACK, P, QUARTERS], BF16, align_bytes=64, bufs=3)
             return grouped_n
 
         def quantise_nodes(g, i, grouped_n):
@@ -115,7 +152,8 @@ def tile_dynamicgraphspatialconv_pa_t_kernel(
 
         def make_tx1(g, k, vector_banks):
             nodes = slice(k * P, (k + 1) * P)
-            grouped_x = stage.tile([P, T_RUN, P, PACK], BF16, align_bytes=64)
+            grouped_x = stage.tile([P, T_RUN, P, PACK], BF16, align_bytes=64, bufs=4)
+            banks = []
             for i in range(T_RUN):
                 tx1_bank = psum.tile([P, PACK, P], F32, tag="tx1", bufs=4)
                 node_codes, node_scales = node[(g, i)]
@@ -129,6 +167,9 @@ def tile_dynamicgraphspatialconv_pa_t_kernel(
                         start=True,
                         stop=True,
                     )
+                banks.append(tx1_bank)
+            for i in EMPTY_ORDER:
+                tx1_bank = banks[i]
                 copy_on(
                     "vector" if i in vector_banks else "scalar",
                     grouped_x[:, i, :, :],
@@ -180,9 +221,20 @@ def tile_dynamicgraphspatialconv_pa_t_kernel(
             )
 
         first_half, second_half = slice(0, P // 2), slice(P // 2, P)
+        sig_place = rows_pool.tile([P, LOADED, P, T], BF16, tag="rows")
+        sym_place = rows_pool.tile([P, LOADED, P, T], BF16, tag="rows")
+        sig_bytes, sym_bytes = (place[:].rearrange("p a n t -> p (a n t)") for place in (sig_place, sym_place))
+        sig, sym = (
+            place[:, : 2 * QUARTERS * N].bitcast(F32).rearrange("p (k v) -> p k v", v=N)
+            for place in (sig_bytes, sym_bytes)
+        )
+        adj_sb, s_rows = (
+            place[:, 2 * QUARTERS * N :].rearrange("p (k v) -> p k v", v=N) for place in (sig_bytes, sym_bytes)
+        )
+        adj_rows = adj_param.rearrange("(k p) v -> p k v", p=P)
+        for k in (0, 2):
+            nc.sync.dma_start(out=adj_sb[:, k : k + 2, :], in_=adj_rows[:, k : k + 2, :])
         load_quarter(0, 0, 2)
-        adj_sb = graph.tile([P, QUARTERS, N], BF16)
-        nc.sync.dma_start(out=adj_sb[:], in_=adj_param.rearrange("(k p) v -> p k v", p=P))
         for k in range(1, QUARTERS):
             load_quarter(0, k)
 
@@ -204,21 +256,18 @@ def tile_dynamicgraphspatialconv_pa_t_kernel(
                     in_=scales[0, 4 * quadrant : 4 * quadrant + 4, :].bitcast(I32),
                 )
         load_quarter(1, 0)
-        load_quarter(1, 1)
 
-        sig = graph.tile([P, QUARTERS, N], F32)
-        sym = graph.tile([P, QUARTERS, N], F32)
         row_sum = graph.tile([P, QUARTERS], F32)
         dis = graph.tile([P, QUARTERS], F32)
         minus_dis = graph.tile([P, QUARTERS], F32)
-        s_rows = graph.tile([P, QUARTERS, N], BF16)
-        s_grouped = graph.tile([P, N, PACK], BF16, align_bytes=64)
+        s_stage = stage.tile([P, PACK, P, QUARTERS], BF16, align_bytes=64, bufs=3, tag="grouped_n")
+        s_grouped = s_stage[:].rearrange("p u m k -> p (u m) k")
         s_codes = keep.tile([P, N], U32, align_bytes=64)
         s_scales = keep.tile([P, N], U8, align_bytes=64)
 
         def sigmoids():
-            nc.scalar.activation(out=sig[:], in_=adj_sb[:], func=ACT.Sigmoid)
             for k in range(QUARTERS):
+                nc.scalar.activation(out=sig[:, k, :], in_=adj_sb[:, k, :], func=ACT.Sigmoid)
                 diagonal_block = sig[:, k, k * P : (k + 1) * P]
                 nc.gpsimd.affine_select(
                     out=diagonal_block,
@@ -271,27 +320,29 @@ def tile_dynamicgraphspatialconv_pa_t_kernel(
                 )
 
         def group_s():
-            nc.vector.tensor_copy(out=s_grouped[:], in_=s_rows[:].rearrange("p k v -> p v k"))
+            nc.vector.tensor_copy(out=s_grouped, in_=s_rows.rearrange("p k v -> p v k"))
 
         def quantise_s():
             nc.vector.quantize_mx(
                 out=s_codes[:].bitcast(FP8X4),
                 scales=s_scales[:],
-                in_=s_grouped[:].rearrange("p v k -> p (v k)"),
+                in_=s_grouped.rearrange("p v k -> p (v k)"),
             )
 
         def turn(step, engines, tags=("tr", "tr")):
             grouped_n = new_grouped_n()
             for h in range(2):
-                turned = turn_nodes(step // T_RUN, step % T_RUN, h, tags[h], 2 if tags[h] == "tr" else 4)
-                empty_turned(turned, grouped_n, h, engines[h])
+                if step < T:
+                    turned = turn_nodes(step // T_RUN, step % T_RUN, h, tags[h], 2 if tags[h] == "tr" else 4)
+                    empty_turned(turned, grouped_n, h, engines[h])
+                else:
+                    spread_rows(step, h, engines[h], grouped_n, "tr", 2)
             return grouped_n
 
+        sigmoids()
         for half in (first_half, second_half):
             group_channels(0, 0, "vector", half)
             group_channels(1, 0, "scalar", half)
-            if half is first_half:
-                sigmoids()
             group_channels(2, 0, "vector", half)
         symmetrise()
         dis_row = spread_degrees()
@@ -301,23 +352,23 @@ def tile_dynamicgraphspatialconv_pa_t_kernel(
         quantise_channels(1, 0)
         group_channels(0, 2, "vector")
         group_channels(1, 2, "scalar")
+        normalise(dis_row)
         group_channels(0, 3, "vector")
         group_channels(1, 3, "scalar")
-        turned_0 = turn(0, ("scalar", "scalar"), ("tr", "tx1"))
-        normalise(dis_row)
         group_s()
         quantise_s()
-        turned_1 = turn(1, ("scalar", "scalar"), ("tr", "tx1"))
+        turned_0 = turn(0, ("scalar", "scalar"), ("tr", "tx1"))
+        turned_1 = turn(1, ("scalar", "vector"), ("tr", "tx1"))
         quantise_nodes(0, 0, turned_0)
-        turned_2 = turn(2, ("scalar", "scalar"), ("tr", "tx1"))
+        turned_2 = turn(2, ("scalar", "vector"), ("tr", "tx1"))
         quantise_nodes(0, 1, turned_1)
         turned_3 = turn(3, ("scalar", "vector"), ("tr", "tx1"))
         quantise_nodes(0, 2, turned_2)
-        waiting_nodes = (0, 3, turned_3)
+        grouped_n = {3: turned_3}
 
         quantise_order = [(0, 1), (0, 2), (0, 3), (1, 1), (1, 2), (1, 3), (2, 0)]
-        waiting_tx1 = None
-        for step in range(-1, GROUPS * QUARTERS + 1):
+        grouped_x, words_x, accs = {}, {}, {}
+        for step in range(-1, GROUPS * QUARTERS + 2):
             g, k = divmod(step, QUARTERS)
             laid, turning = step + 9, step + 5
             lays, turns = 0 <= step and laid < GROUPS * QUARTERS, turning < GROUPS * QUARTERS
@@ -327,27 +378,29 @@ def tile_dynamicgraphspatialconv_pa_t_kernel(
                 vector_banks = (3,)
             else:
                 vector_banks = (1, 3)
-            tx1_words = None
-            if waiting_tx1 is not None:
-                tx1_words = quantise_tx1(waiting_tx1[2])
+            if step - 2 in grouped_x:
+                words_x[step - 2] = quantise_tx1(grouped_x.pop(step - 2))
             if lays:
                 group_channels(laid // QUARTERS, laid % QUARTERS, "vector")
-            grouped_x = None
             if 0 <= step < GROUPS * QUARTERS:
-                grouped_x = make_tx1(g, k, vector_banks)
-            grouped_n = None
+                grouped_x[step] = make_tx1(g, k, vector_banks)
             if turns:
-                grouped_n = turn(turning, ("scalar", "scalar") if lays and k == 3 else ("vector", "scalar"))
-            if tx1_words is not None:
-                acc = add_orders(waiting_tx1[0], waiting_tx1[1], *tx1_words)
-                store_result(waiting_tx1[0], waiting_tx1[1], acc)
-            waiting_tx1 = None if grouped_x is None else (g, k, grouped_x)
-            if waiting_nodes is not None:
-                quantise_nodes(*waiting_nodes)
-            waiting_nodes = None if grouped_n is None else (turning // T_RUN, turning % T_RUN, grouped_n)
+                grouped_n[turning] = turn(turning, ("scalar", "scalar") if lays and k == 3 else ("vector", "scalar"))
+            if step - 2 in words_x:
+                done = step - 2
+                accs[done] = add_orders(done // QUARTERS, done % QUARTERS, *words_x.pop(done))
+            if step - 2 in accs:
+                done = step - 2
+                store_result(done // QUARTERS, done % QUARTERS, accs.pop(done))
+            if turning - 1 in grouped_n:
+                ahead = turning - 1
+                quantise_nodes(ahead // T_RUN, ahead % T_RUN, grouped_n.pop(ahead))
             if quantise_order:
                 quantise_channels(*quantise_order.pop(0))
             if lays:
                 quantise_order.append((laid // QUARTERS, laid % QUARTERS))
-            if 0 <= step < 2:
-                load_quarter(1, step + 2)
+            if 0 <= step < 3:
+                load_quarter(1, step + 1)
+                load_blocks(1, LOADED * step)
+            if step == 3:
+                load_blocks(1, LOADED * step)

@@ -177,20 +177,21 @@ def tile_dynamicgraphspatialconv_pa_t_kernel(
                 )
             return grouped_x
 
-        def quantise_tx1(grouped_x):
+        def quantise_tx1(grouped_x, pieces):
             tx1_codes = stage.tile([P, T_RUN, P], U32, align_bytes=64)
             tx1_scales = stage.tile([P, T_RUN, P], U8, align_bytes=64)
-            nc.vector.quantize_mx(
-                out=tx1_codes[:].rearrange("p t v -> p (t v)").bitcast(FP8X4),
-                scales=tx1_scales[:].rearrange("p t v -> p (t v)"),
-                in_=grouped_x[:].rearrange("p t v u -> p (t v u)"),
-            )
+            for times in pieces:
+                nc.vector.quantize_mx(
+                    out=tx1_codes[:, times, :].rearrange("p t v -> p (t v)").bitcast(FP8X4),
+                    scales=tx1_scales[:, times, :].rearrange("p t v -> p (t v)"),
+                    in_=grouped_x[:, times, :, :].rearrange("p t v u -> p (t v u)"),
+                )
             return tx1_codes, tx1_scales
 
-        def add_orders(g, k, tx1_codes, tx1_scales):
+        def add_orders(g, k, times, tx1_codes, tx1_scales):
             chan_codes, chan_scales = chan[(g, k)]
             acc = psum.tile([P, T_RUN, O], F32, tag="acc", bufs=2)
-            for i in range(T_RUN):
+            for i in range(times.start, times.stop):
                 nc.tensor.matmul_mx(
                     out=acc[:, i, :],
                     lhsT=chan_codes[:, i, :].bitcast(FP8X4),
@@ -211,14 +212,17 @@ def tile_dynamicgraphspatialconv_pa_t_kernel(
                 )
             return acc
 
-        def store_result(g, k, acc):
+        def store_result(g, k, pieces, accs):
             result = res_pool.tile([P, T_RUN, O], F32)
-            nc.scalar.copy(out=result[:], in_=acc[:])
             first = T_RUN * (g % RUNS)
-            nc.sync.dma_start(
-                out=out[g // RUNS, first : first + T_RUN, k * P : (k + 1) * P, :].rearrange("t n o -> n t o"),
-                in_=result[:],
-            )
+            for times, acc in zip(pieces, accs):
+                nc.scalar.copy(out=result[:, times, :], in_=acc[:, times, :])
+                nc.sync.dma_start(
+                    out=out[g // RUNS, first + times.start : first + times.stop, k * P : (k + 1) * P, :].rearrange(
+                        "t n o -> n t o"
+                    ),
+                    in_=result[:, times, :],
+                )
 
         first_half, second_half = slice(0, P // 2), slice(P // 2, P)
         sig_place = rows_pool.tile([P, LOADED, P, T], BF16, tag="rows")
@@ -299,13 +303,7 @@ def tile_dynamicgraphspatialconv_pa_t_kernel(
             nc.gpsimd.tensor_scalar_mul(out=minus_dis[:], in0=dis[:], scalar1=-1.0)
             dis_row = psum.tile([P, QUARTERS, P], F32, tag="acc", bufs=2)
             for k in range(QUARTERS):
-                nc.tensor.matmul(
-                    out=dis_row[:, k, :],
-                    lhsT=dis[:, k : k + 1].to_broadcast([P, P]),
-                    rhs=ident_f32[:],
-                    start=True,
-                    stop=True,
-                )
+                nc.tensor.transpose(dis_row[:, k, :], dis[:, k : k + 1].to_broadcast([P, P]), ident_f32[:])
             return dis_row
 
         def normalise(dis_row):
@@ -367,8 +365,9 @@ def tile_dynamicgraphspatialconv_pa_t_kernel(
         grouped_n = {3: turned_3}
 
         quantise_order = [(0, 1), (0, 2), (0, 3), (1, 1), (1, 2), (1, 3), (2, 0)]
-        grouped_x, words_x, accs = {}, {}, {}
-        for step in range(-1, GROUPS * QUARTERS + 2):
+        grouped_x, words_x = {}, {}
+        last_step = GROUPS * QUARTERS - 1
+        for step in range(-1, last_step + 2):
             g, k = divmod(step, QUARTERS)
             laid, turning = step + 9, step + 5
             lays, turns = 0 <= step and laid < GROUPS * QUARTERS, turning < GROUPS * QUARTERS
@@ -378,20 +377,31 @@ def tile_dynamicgraphspatialconv_pa_t_kernel(
                 vector_banks = (3,)
             else:
                 vector_banks = (1, 3)
-            if step - 2 in grouped_x:
-                words_x[step - 2] = quantise_tx1(grouped_x.pop(step - 2))
+            if step < last_step:
+                finished = [step - 2]
+            elif step == last_step:
+                finished = [step - 2, step - 1]
+            else:
+                finished = [step - 1]
+            if step <= last_step:
+                pieces = (slice(0, T_RUN),)
+            else:
+                pieces = (slice(0, T_RUN // 2), slice(T_RUN // 2, T_RUN))
+            for done in finished:
+                if done in grouped_x:
+                    words_x[done] = quantise_tx1(grouped_x.pop(done), pieces)
             if lays:
                 group_channels(laid // QUARTERS, laid % QUARTERS, "vector")
             if 0 <= step < GROUPS * QUARTERS:
                 grouped_x[step] = make_tx1(g, k, vector_banks)
             if turns:
-                grouped_n[turning] = turn(turning, ("scalar", "scalar") if lays and k == 3 else ("vector", "scalar"))
-            if step - 2 in words_x:
-                done = step - 2
-                accs[done] = add_orders(done // QUARTERS, done % QUARTERS, *words_x.pop(done))
-            if step - 2 in accs:
-                done = step - 2
-                store_result(done // QUARTERS, done % QUARTERS, accs.pop(done))
+                scalar_alone = lays and (k == 3 or (turning >= T and k == 1))
+                grouped_n[turning] = turn(turning, ("scalar" if scalar_alone else "vector", "scalar"))
+            for done in finished:
+                if done in words_x:
+                    tx1_words = words_x.pop(done)
+                    accs = [add_orders(done // QUARTERS, done % QUARTERS, times, *tx1_words) for times in pieces]
+                    store_result(done // QUARTERS, done % QUARTERS, pieces, accs)
             if turning - 1 in grouped_n:
                 ahead = turning - 1
                 quantise_nodes(ahead // T_RUN, ahead % T_RUN, grouped_n.pop(ahead))

@@ -44,6 +44,10 @@ def tile_dynamicgraphspatialconv_pa_t_kernel(
 
         ident_f32 = keep.tile([P, P], F32)
         make_identity(nc, ident_f32[:])
+        off_diagonal = keep.tile([P, P], F32)
+        nc.gpsimd.tensor_scalar(
+            out=off_diagonal[:], in0=ident_f32[:], scalar1=-1.0, scalar2=1.0, op0=ALU.mult, op1=ALU.add
+        )
         spread = keep.tile([P, P], BF16)
         nc.gpsimd.tensor_copy(
             out=spread[:].rearrange("p (u m k) -> p m u k", u=PACK, k=QUARTERS),
@@ -245,8 +249,9 @@ def tile_dynamicgraphspatialconv_pa_t_kernel(
         w_codes = keep.tile([P, 2, PACK * O], U8, align_bytes=64)
         w_scales = keep.tile([P, 2, O], U8, align_bytes=64)
         nc.gpsimd.memset(w_scales[:].rearrange("p w o -> p (w o)").bitcast(I32), 0)
-        minus_half = graph.tile([P, QUARTERS], F32)
-        nc.gpsimd.memset(minus_half[:], -0.5)
+        ones = graph.tile([P, 1], F32)
+        nc.gpsimd.memset(ones[:], 1.0)
+        root_of_one = graph.tile([P, 1], F32)
         for w, (words, scales) in enumerate(
             ((w_cheb0_words, w_cheb0_scales), (w_cheb1_words, w_cheb1_scales))
         ):
@@ -262,6 +267,7 @@ def tile_dynamicgraphspatialconv_pa_t_kernel(
         load_quarter(1, 0)
 
         row_sum = graph.tile([P, QUARTERS], F32)
+        root = graph.tile([P, QUARTERS], F32)
         dis = graph.tile([P, QUARTERS], F32)
         minus_dis = graph.tile([P, QUARTERS], F32)
         s_stage = stage.tile([P, PACK, P, QUARTERS], BF16, align_bytes=64, bufs=3, tag="grouped_n")
@@ -272,16 +278,9 @@ def tile_dynamicgraphspatialconv_pa_t_kernel(
         def sigmoids():
             for k in range(QUARTERS):
                 nc.scalar.activation(out=sig[:, k, :], in_=adj_sb[:, k, :], func=ACT.Sigmoid)
+            for k in range(QUARTERS):
                 diagonal_block = sig[:, k, k * P : (k + 1) * P]
-                nc.gpsimd.affine_select(
-                    out=diagonal_block,
-                    in_=diagonal_block,
-                    compare_op=ALU.not_equal,
-                    fill=0.0,
-                    base=0,
-                    pattern=[[-1, P]],
-                    channel_multiplier=1,
-                )
+                nc.vector.tensor_tensor(out=diagonal_block, in0=diagonal_block, in1=off_diagonal[:], op=ALU.mult)
 
         def symmetrise():
             for k in range(QUARTERS):
@@ -298,9 +297,12 @@ def tile_dynamicgraphspatialconv_pa_t_kernel(
                     accum_out=row_sum[:, k : k + 1],
                 )
 
+        def take_roots():
+            nc.scalar.activation(out=root[:], in_=row_sum[:], func=ACT.Sqrt)
+
         def spread_degrees():
-            nc.gpsimd.tensor_tensor(out=dis[:], in0=row_sum[:], in1=minus_half[:], op=ALU.pow)
-            nc.gpsimd.tensor_scalar_mul(out=minus_dis[:], in0=dis[:], scalar1=-1.0)
+            nc.vector.reciprocal(out=dis[:], in_=root[:])
+            nc.scalar.mul(out=minus_dis[:], in_=dis[:], mul=-1.0)
             dis_row = psum.tile([P, QUARTERS, P], F32, tag="acc", bufs=2)
             for k in range(QUARTERS):
                 nc.tensor.transpose(dis_row[:, k, :], dis[:, k : k + 1].to_broadcast([P, P]), ident_f32[:])
@@ -342,10 +344,13 @@ def tile_dynamicgraphspatialconv_pa_t_kernel(
             group_channels(0, 0, "vector", half)
             group_channels(1, 0, "scalar", half)
             group_channels(2, 0, "vector", half)
+        nc.scalar.activation(out=root_of_one[:], in_=ones[:], func=ACT.Sqrt)
         symmetrise()
-        dis_row = spread_degrees()
+        group_channels(1, 1, "scalar", first_half)
+        take_roots()
         group_channels(0, 1, "vector")
-        group_channels(1, 1, "scalar")
+        group_channels(1, 1, "scalar", second_half)
+        dis_row = spread_degrees()
         quantise_channels(0, 0)
         quantise_channels(1, 0)
         group_channels(0, 2, "vector")

from contextlib import ExitStack

import concourse.mybir as mybir
from concourse.masks import make_identity

BF16 = mybir.dt.bfloat16
F32 = mybir.dt.float32
I32 = mybir.dt.int32
U32 = mybir.dt.uint32
U8 = mybir.dt.uint8
FP8X4 = mybir.dt.float8_e4m3fn_x4
ACT = mybir.ActivationFunctionType
ALU = mybir.AluOpType

P = 128
PACK = 4
B, C, N, T, O = 2, 512, 512, 12, 128
QUARTERS = N // P
T_RUN = 4
RUNS = T // T_RUN
GROUPS = B * RUNS
BLOCKS = C * QUARTERS // P
LOADED = 4
BANKED = 8
GROUPED = 9
EMPTY_ORDER = (1, 0, 3, 2)

FLOPS = 2 * B * T * (N * N * C + 2 * N * C * O)


def tile_dynamicgraphspatialconv_pa_t_kernel(
    tc, x, adj_param, w_cheb0_words, w_cheb0_scales, w_cheb1_words, w_cheb1_scales, out
):
    nc = tc.nc
    with ExitStack() as ctx:
        keep = ctx.enter_context(tc.tile_pool(name="keep", bufs=1))
        graph = ctx.enter_context(tc.tile_pool(name="graph", bufs=1))
        raw_pool = ctx.enter_context(tc.tile_pool(name="raw", bufs=5))
        rows_pool = ctx.enter_context(tc.tile_pool(name="rows", bufs=BLOCKS // LOADED))
        stage = ctx.enter_context(tc.tile_pool(name="stage", bufs=3))
        code_pool = ctx.enter_context(tc.tile_pool(name="codes", bufs=6))
        res_pool = ctx.enter_context(tc.tile_pool(name="res", bufs=3))
        psum = ctx.enter_context(tc.psum_pool(name="psum", bufs=2))

        ident_f32 = keep.tile([P, P], F32)
        make_identity(nc, ident_f32[:])
        off_diagonal = keep.tile([P, P], F32)
        nc.gpsimd.tensor_scalar(
            out=off_diagonal[:], in0=ident_f32[:], scalar1=-1.0, scalar2=1.0, op0=ALU.mult, op1=ALU.add
        )
        spread = keep.tile([P, P], BF16)
        nc.gpsimd.tensor_copy(
            out=spread[:].rearrange("p (u m k) -> p m u k", u=PACK, k=QUARTERS),
            in_=ident_f32[:].rearrange("p (m u k) -> p m u k", u=PACK, k=QUARTERS),
        )
        ctx.enter_context(tc.manual_schedule())

        def copy_on(engine, dst, src):
            if engine == "vector":
                nc.vector.tensor_copy(out=dst, in_=src)
            else:
                nc.scalar.copy(out=dst, in_=src)

        raw = {}

        def load_quarter(b, k, pieces=1):
            raw_c = raw_pool.tile([P, PACK, P, T], BF16)
            source = x[b].rearrange("(p j) (k n) t -> k p j n t", j=PACK, k=QUARTERS)
            raw[(b, k)] = raw_c
            for n in range(0, P, P // pieces):
                nodes = slice(n, n + P // pieces)
                nc.sync.dma_start(
                    out=raw_c[:, :, nodes, :].rearrange("p j n t -> p j (n t)"),
                    in_=source[k][:, :, nodes, :].rearrange("p j n t -> p j (n t)"),
                )

        rows = {}

        def load_blocks(b, first):
            rows_b = rows_pool.tile([P, LOADED, P, T], BF16, tag="rows")
            source = x[b].rearrange("(a c) (k n) t -> (c k) a (n t)", a=BLOCKS, k=QUARTERS)
            nc.sync.dma_start(
                out=rows_b[:].rearrange("q a n t -> q a (n t)"), in_=source[:, first : first + LOADED, :]
            )
            for a in range(LOADED):
                rows[(b, first + a)] = rows_b[:, a, :, :]

        grouped = {}
        chan = {}

        def group_channels(g, k, engine, nodes=slice(0, P)):
            first = T_RUN * (g % RUNS)
            if nodes.start == 0:
                grouped_c = stage.tile([P, T_RUN, P, PACK], BF16, align_bytes=64, bufs=GROUPED)
                grouped[(g, k)] = grouped_c
            copy_on(
                engine,
                grouped[(g, k)][:, :, nodes, :].rearrange("p t n j -> p n j t"),
                raw[(g // RUNS, k)][:, :, nodes, first : first + T_RUN].rearrange("p j n t -> p n j t"),
            )

        def quantise_channels(g, k):
            chan_codes = code_pool.tile([P, T_RUN, P], U32, align_bytes=64, bufs=11)
            chan_scales = code_pool.tile([P, T_RUN, P], U8, align_bytes=64, bufs=11)
            nc.vector.quantize_mx(
                out=chan_codes[:].rearrange("p t n -> p (t n)").bitcast(FP8X4),
                scales=chan_scales[:].rearrange("p t n -> p (t n)"),
                in_=grouped[(g, k)][:].rearrange("p t n j -> p (t n j)"),
            )
            chan[(g, k)] = (chan_codes, chan_scales)

        node = {}

        def turn_nodes(g, i, h, tag, bufs):
            turned = psum.tile([P, QUARTERS, P], F32, tag=tag, bufs=bufs)
            for k in range(QUARTERS):
                words = grouped[(g, k)][:].rearrange("p t n j -> p (t n j)").bitcast(F32)
                words = words.rearrange("p (t n h) -> p t n h", t=T_RUN, h=2)
                nc.tensor.transpose(turned[:, k, :], words[:, i, :, h], ident_f32[:])
            return turned

        def empty_turned(turned, grouped_n, h, engine):
            single_channels = turned[:].rearrange("p k m -> p (k m)").bitcast(BF16)
            single_channels = single_channels.rearrange("p (k m e) -> p e m k", k=QUARTERS, e=2)
            copy_on(engine, grouped_n[:, 2 * h : 2 * h + 2, :, :], single_channels)

        def spread_rows(time, half, engine, grouped_n, tag, bufs):
            turned = psum.tile([P, BANKED, P], BF16, tag=tag, bufs=bufs)
            for a in range(BANKED):
                nc.tensor.matmul(
                    out=turned[:, a, :],
                    lhsT=rows[(time // T, BANKED * half + a)][:, :, time % T],
                    rhs=spread[:],
                    start=True,
                    stop=True,
                )
            copy_on(
                engine,
                grouped_n[:, :, half * P // 2 : (half + 1) * P // 2, :].rearrange("p u (a m) k -> p u a (m k)", a=BANKED),
                turned[:].rearrange("p a (u w) -> p u a w", u=PACK),
            )

        def new_grouped_n():
            grouped_n = stage.tile([P, PACK, P, QUARTERS], BF16, align_bytes=64, bufs=3)
            return grouped_n

        def quantise_nodes(g, i, grouped_n):
            node_codes = code_pool.tile([P, PACK, P], U32, align_bytes=64)
            node_scales = code_pool.tile([P, PACK, P], U8, align_bytes=64)
            nc.vector.quantize_mx(
                out=node_codes[:].rearrange("p u m -> p (u m)").bitcast(FP8X4),
                scales=node_scales[:].rearrange("p u m -> p (u m)"),
                in_=grouped_n[:].rearrange("p u m k -> p (u m k)"),
            )
            node[(g, i)] = (node_codes, node_scales)

        def make_tx1(g, k, vector_banks):
            nodes = slice(k * P, (k + 1) * P)
            grouped_x = stage.tile([P, T_RUN, P, PACK], BF16, align_bytes=64, bufs=4)
            banks = []
            for i in range(T_RUN):
                tx1_bank = psum.tile([P, PACK, P], F32, tag="tx1", bufs=4)
                node_codes, node_scales = node[(g, i)]
                for u in range(PACK):
                    nc.tensor.matmul_mx(
                        out=tx1_bank[:, u, :],
                        lhsT=node_codes[:, u, :].bitcast(FP8X4),
                        lhsT_scale=node_scales[:, u, :],
                        rhs=s_codes[:, nodes].bitcast(FP8X4),
                        rhs_scale=s_scales[:, nodes],
                        start=True,
                        stop=True,
                    )
                banks.append(tx1_bank)
            for i in EMPTY_ORDER:
                tx1_bank = banks[i]
                copy_on(
                    "vector" if i in vector_banks else "scalar",
                    grouped_x[:, i, :, :],
                    tx1_bank[:].rearrange("p u v -> p v u"),
                )
            return grouped_x

        def quantise_tx1(grouped_x, pieces):
            tx1_codes = stage.tile([P, T_RUN, P], U32, align_bytes=64)
            tx1_scales = stage.tile([P, T_RUN, P], U8, align_bytes=64)
            for times in pieces:
                nc.vector.quantize_mx(
                    out=tx1_codes[:, times, :].rearrange("p t v -> p (t v)").bitcast(FP8X4),
                    scales=tx1_scales[:, times, :].rearrange("p t v -> p (t v)"),
                    in_=grouped_x[:, times, :, :].rearrange("p t v u -> p (t v u)"),
                )
            return tx1_codes, tx1_scales

        def add_orders(g, k, times, tx1_codes, tx1_scales):
            chan_codes, chan_scales = chan[(g, k)]
            acc = psum.tile([P, T_RUN, O], F32, tag="acc", bufs=2)
            for i in range(times.start, times.stop):
                nc.tensor.matmul_mx(
                    out=acc[:, i, :],
                    lhsT=chan_codes[:, i, :].bitcast(FP8X4),
                    lhsT_scale=chan_scales[:, i, :],
                    rhs=w_codes[:, 0, :].bitcast(FP8X4),
                    rhs_scale=w_scales[:, 0, :],
                    start=True,
                    stop=False,
                )
                nc.tensor.matmul_mx(
                    out=acc[:, i, :],
                    lhsT=tx1_codes[:, i, :].bitcast(FP8X4),
                    lhsT_scale=tx1_scales[:, i, :],
                    rhs=w_codes[:, 1, :].bitcast(FP8X4),
                    rhs_scale=w_scales[:, 1, :],
                    start=False,
                    stop=True,
                )
            return acc

        def store_result(g, k, pieces, accs):
            result = res_pool.tile([P, T_RUN, O], F32)
            first = T_RUN * (g % RUNS)
            for times, acc in zip(pieces, accs):
                nc.scalar.copy(out=result[:, times, :], in_=acc[:, times, :])
                nc.sync.dma_start(
                    out=out[g // RUNS, first + times.start : first + times.stop, k * P : (k + 1) * P, :].rearrange(
                        "t n o -> n t o"
                    ),
                    in_=result[:, times, :],
                )

        first_half, second_half = slice(0, P // 2), slice(P // 2, P)
        sig_place = rows_pool.tile([P, LOADED, P, T], BF16, tag="rows")
        sym_place = rows_pool.tile([P, LOADED, P, T], BF16, tag="rows")
        sig_bytes, sym_bytes = (place[:].rearrange("p a n t -> p (a n t)") for place in (sig_place, sym_place))
        sig, sym = (
            place[:, : 2 * QUARTERS * N].bitcast(F32).rearrange("p (k v) -> p k v", v=N)
            for place in (sig_bytes, sym_bytes)
        )
        adj_sb, s_rows = (
            place[:, 2 * QUARTERS * N :].rearrange("p (k v) -> p k v", v=N) for place in (sig_bytes, sym_bytes)
        )
        adj_rows = adj_param.rearrange("(k p) v -> p k v", p=P)
        for k in (0, 2):
            nc.sync.dma_start(out=adj_sb[:, k : k + 2, :], in_=adj_rows[:, k : k + 2, :])
        load_quarter(0, 0, 2)
        for k in range(1, QUARTERS):
            load_quarter(0, k)

        w_codes = keep.tile([P, 2, PACK * O], U8, align_bytes=64)
        w_scales = keep.tile([P, 2, O], U8, align_bytes=64)
        nc.gpsimd.memset(w_scales[:].rearrange("p w o -> p (w o)").bitcast(I32), 0)
        ones = graph.tile([P, 1], F32)
        nc.gpsimd.memset(ones[:], 1.0)
        root_of_one = graph.tile([P, 1], F32)
        for w, (words, scales) in enumerate(
            ((w_cheb0_words, w_cheb0_scales), (w_cheb1_words, w_cheb1_scales))
        ):
            nc.sync.dma_start(
                out=w_codes[:, w, :].bitcast(I32),
                in_=words[0].rearrange("p o j -> p (o j)").bitcast(I32),
            )
            for quadrant in range(4):
                nc.sync.dma_start(
                    out=w_scales[32 * quadrant : 32 * quadrant + 4, w, :].bitcast(I32),
                    in_=scales[0, 4 * quadrant : 4 * quadrant + 4, :].bitcast(I32),
                )
        load_quarter(1, 0)

        row_sum = graph.tile([P, QUARTERS], F32)
        root = graph.tile([P, QUARTERS], F32)
        dis = graph.tile([P, QUARTERS], F32)
        minus_dis = graph.tile([P, QUARTERS], F32)
        s_stage = stage.tile([P, PACK, P, QUARTERS], BF16, align_bytes=64, bufs=3, tag="grouped_n")
        s_grouped = s_stage[:].rearrange("p u m k -> p (u m) k")
        s_codes = keep.tile([P, N], U32, align_bytes=64)
        s_scales = keep.tile([P, N], U8, align_bytes=64)

        def sigmoids():
            for k in range(QUARTERS):
                nc.scalar.activation(out=sig[:, k, :], in_=adj_sb[:, k, :], func=ACT.Sigmoid)
            for k in range(QUARTERS):
                diagonal_block = sig[:, k, k * P : (k + 1) * P]
                nc.vector.tensor_tensor(out=diagonal_block, in0=diagonal_block, in1=off_diagonal[:], op=ALU.mult)

        def symmetrise():
            for k in range(QUARTERS):
                sig_t = psum.tile([P, QUARTERS, P], F32, tag="tx1", bufs=4)
                for kv in range(QUARTERS):
                    nc.tensor.transpose(sig_t[:, kv, :], sig[:, kv, k * P : (k + 1) * P], ident_f32[:])
                nc.vector.scalar_tensor_tensor(
                    out=sym[:, k, :],
                    in0=sig[:, k, :],
                    scalar=1.0,
                    in1=sig_t[:].rearrange("p k v -> p (k v)"),
                    op0=ALU.mult,
                    op1=ALU.add,
                    accum_out=row_sum[:, k : k + 1],
                )

        def take_roots():
            nc.scalar.activation(out=root[:], in_=row_sum[:], func=ACT.Sqrt)

        def spread_degrees():
            nc.vector.reciprocal(out=dis[:], in_=root[:])
            nc.scalar.mul(out=minus_dis[:], in_=dis[:], mul=-1.0)
            dis_row = psum.tile([P, QUARTERS, P], F32, tag="acc", bufs=2)
            for k in range(QUARTERS):
                nc.tensor.transpose(dis_row[:, k, :], dis[:, k : k + 1].to_broadcast([P, P]), ident_f32[:])
            return dis_row

        def normalise(dis_row):
            for k in range(QUARTERS):
                nc.vector.scalar_tensor_tensor(
                    out=s_rows[:, k, :],
                    in0=sym[:, k, :],
                    scalar=minus_dis[:, k : k + 1],
                    in1=dis_row[:].rearrange("p k v -> p (k v)"),
                    op0=ALU.mult,
                    op1=ALU.mult,
                )

        def group_s():
            nc.vector.tensor_copy(out=s_grouped, in_=s_rows.rearrange("p k v -> p v k"))

        def quantise_s():
            nc.vector.quantize_mx(
                out=s_codes[:].bitcast(FP8X4),
                scales=s_scales[:],
                in_=s_grouped.rearrange("p v k -> p (v k)"),
            )

        def turn(step, engines, tags=("tr", "tr")):
            grouped_n = new_grouped_n()
            for h in range(2):
                if step < T:
                    turned = turn_nodes(step // T_RUN, step % T_RUN, h, tags[h], 2 if tags[h] == "tr" else 4)
                    empty_turned(turned, grouped_n, h, engines[h])
                else:
                    spread_rows(step, h, engines[h], grouped_n, "tr", 2)
            return grouped_n

        sigmoids()
        for half in (first_half, second_half):
            group_channels(0, 0, "vector", half)
            group_channels(1, 0, "scalar", half)
            group_channels(2, 0, "vector", half)
        nc.scalar.activation(out=root_of_one[:], in_=ones[:], func=ACT.Sqrt)
        symmetrise()
        group_channels(1, 1, "scalar", first_half)
        take_roots()
        group_channels(0, 1, "vector")
        group_channels(1, 1, "scalar", second_half)
        dis_row = spread_degrees()
        quantise_channels(0, 0)
        quantise_channels(1, 0)
        group_channels(0, 2, "vector")
        group_channels(1, 2, "scalar")
        normalise(dis_row)
        group_channels(0, 3, "vector")
        group_channels(1, 3, "scalar")
        group_s()
        quantise_s()
        turned_0 = turn(0, ("scalar", "scalar"), ("tr", "tx1"))
        turned_1 = turn(1, ("scalar", "vector"), ("tr", "tx1"))
        quantise_nodes(0, 0, turned_0)
        turned_2 = turn(2, ("scalar", "vector"), ("tr", "tx1"))
        quantise_nodes(0, 1, turned_1)
        turned_3 = turn(3, ("scalar", "vector"), ("tr", "tx1"))
        quantise_nodes(0, 2, turned_2)
        grouped_n = {3: turned_3}

        quantise_order = [(0, 1), (0, 2), (0, 3), (1, 1), (1, 2), (1, 3), (2, 0)]
        grouped_x, words_x = {}, {}
        last_step = GROUPS * QUARTERS - 1
        for step in range(-1, last_step + 2):
            g, k = divmod(step, QUARTERS)
            laid, turning = step + 9, step + 5
            lays, turns = 0 <= step and laid < GROUPS * QUARTERS, turning < GROUPS * QUARTERS
            if lays:
                vector_banks = ()
            elif turns:
                vector_banks = (3,)
            else:
                vector_banks = (1, 3)
            if step < last_step:
                finished = [step - 2]
            elif step == last_step:
                finished = [step - 2, step - 1]
            else:
                finished = [step - 1]
            if step <= last_step:
                pieces = (slice(0, T_RUN),)
            else:
                pieces = (slice(0, T_RUN // 2), slice(T_RUN // 2, T_RUN))
            for done in finished:
                if done in grouped_x:
                    words_x[done] = quantise_tx1(grouped_x.pop(done), pieces)
            if lays:
                group_channels(laid // QUARTERS, laid % QUARTERS, "vector")
            if 0 <= step < GROUPS * QUARTERS:
                grouped_x[step] = make_tx1(g, k, vector_banks)
            if turns:
                scalar_alone = lays and (k == 3 or (turning >= T and k == 1))
                grouped_n[turning] = turn(turning, ("scalar" if scalar_alone else "vector", "scalar"))
            for done in finished:
                if done in words_x:
                    tx1_words = words_x.pop(done)
                    accs = [add_orders(done // QUARTERS, done % QUARTERS, times, *tx1_words) for times in pieces]
                    store_result(done // QUARTERS, done % QUARTERS, pieces, accs)
            if turning - 1 in grouped_n:
                ahead = turning - 1
                quantise_nodes(ahead // T_RUN, ahead % T_RUN, grouped_n.pop(ahead))
            if quantise_order:
                quantise_channels(*quantise_order.pop(0))
            if lays:
                quantise_order.append((laid // QUARTERS, laid % QUARTERS))
            if 0 <= step < 3:
                load_quarter(1, step + 1)
                load_blocks(1, LOADED * step)
            if step == 3:
                load_blocks(1, LOADED * step)
